import numpy as np
import ml_dtypes


def mxq(x, axis, fmt="e4m3"):
    dtype, down = {"e4m3": (ml_dtypes.float8_e4m3fn, 7), "e5m2": (ml_dtypes.float8_e5m2, 14)}[fmt]
    v = np.moveaxis(np.asarray(x, np.float32).astype(ml_dtypes.bfloat16).astype(np.float64), axis, -1)
    blocks = v.reshape(v.shape[:-1] + (-1, 32))
    amax = np.abs(blocks).max(-1, keepdims=True)
    byte = np.maximum(np.where(amax > 0, np.frexp(amax)[1] - 1 + 127, 0) - down, 1)
    scale = np.exp2(byte - 127.0)
    codes = (blocks / scale).astype(np.float32).astype(dtype).astype(np.float64)
    return np.moveaxis((codes * scale).reshape(v.shape), -1, axis)


WIDE = False


def mx_kscale(k):
    if not WIDE:
        return np.ones(k)
    levels = np.array([10, -10, 5, -5, 0])
    if k % 512:
        return np.exp2(np.random.permutation(np.resize(levels, k // 32))).repeat(32)
    a = np.empty((k // 512, 16))
    for p in range(k // 512):
        a[p, :8] = np.random.permutation(np.resize(levels, 8))
        for g in range(8):
            far = levels[np.abs(levels - a[p, g]) >= 10]
            a[p, g + 8] = far[np.random.randint(len(far))]
    return np.exp2(a.ravel()).repeat(32)


BF16 = ml_dtypes.bfloat16


def bf(x):
    return np.asarray(x, np.float32).astype(BF16)


def f64(x):
    return np.asarray(x).astype(np.float64)


B, STACK, TUBE, CH, IMG, PATCH, EMBED = 4, 16, 2, 1, 96, 16, 1024
GH = IMG // PATCH
GW = IMG // PATCH
GD = STACK // TUBE
K = TUBE * CH * PATCH * PATCH


def _sincos_1d(dim, pos):
    omega = 1.0 / (10000.0 ** (np.arange(dim // 2, dtype=np.float64) / (dim / 2.0)))
    out = pos[:, None].astype(np.float64) * omega[None, :]
    return np.concatenate([np.sin(out), np.cos(out)], axis=1)


def get_3d_sincos_pos_embed(grid_h, grid_w, grid_depth, embed_dim):
    dim_t = embed_dim // 4
    dim_s = embed_dim - dim_t
    emb_t = _sincos_1d(dim_t, np.arange(grid_depth))
    emb_h = _sincos_1d(dim_s // 2, np.arange(grid_h))
    emb_w = _sincos_1d(dim_s - dim_s // 2, np.arange(grid_w))
    emb_hw = np.concatenate([np.repeat(emb_h, grid_w, axis=0), np.tile(emb_w, (grid_h, 1))], axis=1)
    ns = grid_h * grid_w
    return np.concatenate([np.repeat(emb_t, ns, axis=0), np.tile(emb_hw, (grid_depth, 1))], axis=1)


def setup_inputs():
    s = mx_kscale(K)
    sv = s.reshape(TUBE, CH, PATCH, PATCH)[:, :, None, :, None, :]
    video = np.random.standard_normal((B, GD, TUBE, CH, GH, PATCH, GW, PATCH)) * sv
    return {"video": bf(video.reshape(B, STACK, CH, IMG, IMG)),
            "W": bf(np.random.standard_normal((EMBED, K)) / np.sqrt(K) / s[None, :]),
            "b": bf(np.random.standard_normal(EMBED) * 0.3),
            "pos_embed": bf(get_3d_sincos_pos_embed(GH, GW, GD, EMBED)[None])}


def reference(video, W, b, pos_embed):
    video = f64(video)
    B_, T, C, H, W_ = video.shape
    p = PATCH
    gh, gw = H // p, W_ // p
    ns = gh * gw
    x = video.reshape(B_ * T, C, gh, p, gw, p)
    x = x.transpose(0, 2, 4, 1, 3, 5)
    x = x.reshape(B_, T, ns, C * p * p)
    x = x.reshape(B_, GD, TUBE, ns, C * p * p)
    x = x.transpose(0, 1, 3, 2, 4)
    tubelets = x.reshape(B_, GD * ns, TUBE * C * p * p)
    tokens = (mxq(tubelets, 2, "e4m3") @ mxq(f64(W), 1, "e4m3").T) + f64(b) + f64(pos_embed)
    return tokens

@@ -1,0 +1,273 @@
+from contextlib import ExitStack
+
+import concourse.mybir as mybir
+from concourse.masks import make_identity
+
+F32 = mybir.dt.float32
+BF16 = mybir.dt.bfloat16
+U32 = mybir.dt.uint32
+U8 = mybir.dt.uint8
+FP8X4 = mybir.dt.float8_e4m3fn_x4
+ADD = mybir.AluOpType.add
+P = 128
+FLOPS = 2 * 1152 * 512 * 1024
+
+
+def tile_tubeletembedding_kernel(tc, video, W, b, pos_embed, out):
+    nc = tc.nc
+    with ExitStack() as ctx:
+        keep = ctx.enter_context(tc.tile_pool(name="keep", bufs=1))
+        psum = ctx.enter_context(tc.psum_pool(name="psum", bufs=8))
+        ctx.enter_context(tc.manual_schedule())
+
+        vid = video.rearrange("b (d t) o (h c y) x -> t c (b d) h (o y x)", t=2, h=2, c=3, y=16)
+        wv = W.rearrange("(h p a) k -> p h a k", h=2, a=4)
+        pv = pos_embed.rearrange("o (s r) e -> (o s) r e", r=18)
+        ov = out.rearrange("b (s r) e -> b s r e", r=18)
+        on = out.rearrange("b (s r) e -> (b s) r e", r=18)
+
+        ident = keep.tile([P, P], F32)
+        make_identity(nc, ident[:])
+        z = keep.tile([P, 1024], BF16)
+        nc.vector.memset(z[:], 0.0)
+
+        v_sb = keep.tile([P, 2, 1536], BF16)
+        w_sb = keep.tile([P, 2, 4, 512], BF16)
+        pos_sb = [keep.tile([P, 1024], BF16, name="pos%d" % g) for g in range(2)]
+        for t in range(2):
+            for c in range(2):
+                nc.sync.dma_start(out=v_sb[c:P:2, t, :], in_=vid[t, c])
+        nc.sync.dma_start(out=w_sb[:, 0, 0:2, :], in_=wv[:, 0, 0:2, :])
+        nc.sync.dma_start(out=w_sb[:, 0, 2:4, :], in_=wv[:, 0, 2:4, :])
+        nc.sync.dma_start(out=z[32:33, :], in_=b.unsqueeze(0))
+        nc.sync.dma_start(out=z[0:32, :], in_=pv[:, 8:10, :])
+        nc.sync.dma_start(out=pos_sb[0][:], in_=pv[:, 0:8, :])
+        nc.sync.dma_start(out=w_sb[:, 1, :, :], in_=wv[:, 1, :, :])
+
+        perm = keep.tile([P, P], F32)
+        nc.vector.tensor_copy(
+            out=perm[:].rearrange("p (c x) -> p c x", c=2),
+            in_=ident[:].rearrange("p (x c) -> p c x", c=2),
+        )
+        sel_n = keep.tile([P, P], BF16)
+        nc.vector.tensor_tensor(
+            out=sel_n[:].rearrange("p (c q) -> p c q", c=4),
+            in0=ident[:, 0:32].unsqueeze(1).to_broadcast([P, 4, 32]),
+            in1=ident[:, 32:33].unsqueeze(1).to_broadcast([P, 4, 32]),
+            op=ADD,
+        )
+        sel_b = keep.tile([P, P], BF16)
+        nc.vector.tensor_copy(out=sel_b[:], in_=ident[:, 32:33].to_broadcast([P, P]))
+
+        v2 = [keep.tile([P, 3072], BF16, name="v2_%d" % s) for s in range(2)]
+        grp = keep.tile([P, 4608], BF16, align_bytes=64)
+        grpw = grp[:].bitcast(F32)
+        tokc = keep.tile([P, 1152], U32, align_bytes=64)
+        toks = keep.tile([P, 1152], U8, align_bytes=64)
+        gw = keep.tile([P, 4096], BF16, align_bytes=64)
+        gww = gw[:].bitcast(F32)
+        wc = keep.tile([P, 1024], U32, align_bytes=64)
+        ws = keep.tile([P, 1024], U8, align_bytes=64)
+        posb = [keep.tile([P, 1024], F32, name="posb%d" % g) for g in range(3)]
+        o_sb = [keep.tile([P, 1024], F32, name="o%d" % t) for t in range(9)]
+        bbcs = keep.tile([P, 1024], F32)
+        bbc = {}
+        accs = {}
+
+        def half(h):
+            return slice(h * 512, (h + 1) * 512)
+
+        def copy_out(eng, dst, src):
+            if eng == "V":
+                nc.vector.tensor_copy(out=dst, in_=src)
+            else:
+                nc.scalar.copy(out=dst, in_=src)
+
+        def bbc_mm(h):
+            bbc[h] = psum.tile([P, 512], F32, tag="bank", name="bbc%d" % h)
+            nc.tensor.matmul(out=bbc[h][:], lhsT=sel_b[:], rhs=z[:, half(h)], start=True, stop=True)
+
+        def pn_mm(h):
+            pn = psum.tile([P, 512], F32, tag="bank", name="pn%d" % h)
+            nc.tensor.matmul(out=pn[:], lhsT=sel_n[:], rhs=z[:, half(h)], start=True, stop=True)
+            nc.scalar.copy(out=posb[2][:, half(h)], in_=pn[:])
+
+        def bbc_copy(h):
+            nc.scalar.copy(out=bbcs[:, half(h)], in_=bbc[h][:])
+
+        def make_posb(g, h):
+            nc.gpsimd.tensor_tensor(out=posb[g][:, half(h)], in0=pos_sb[g][:, half(h)], in1=bbcs[:, half(h)], op=ADD)
+
+        def regroup(s, t):
+            dst = v2[s][:].bitcast(F32).rearrange("p (j u t y x) -> p t j u y x", j=6, u=2, t=2, y=16)
+            src = v_sb[:, t, :].bitcast(F32).rearrange("p (y j x u) -> p j u y x", y=16, j=6, u=2)
+            for u in range(2):
+                nc.vector.tensor_copy(out=dst[:, t, :, u], in_=src[:, :, u])
+
+        def tok_a(j0):
+            pt = psum.tile([P, 512], F32, tag="bank", name="pa%d" % j0)
+            vw = v2[0][:].bitcast(F32)
+            for i in range(4):
+                r = 2 * j0 + i
+                nc.tensor.transpose(pt[:, i * P:(i + 1) * P], vw[:, r * P:(r + 1) * P], perm[:])
+            return pt[:].rearrange("p (j u c x) -> p c x j u", j=2, u=2, c=2)
+
+        def tok_b(j0):
+            pt = psum.tile([P, 512], F32, tag="bank", name="pb%d" % j0)
+            vw = v2[1][:].bitcast(F32)
+            for i in range(4):
+                r = 2 * j0 + i
+                nc.tensor.transpose(pt[:, i * 64:i * 64 + P], vw[:, r * P:(r + 1) * P], perm[:])
+            return pt[:, 0:256].rearrange("p (j u x) -> p x j u", j=2, u=2)
+
+        g_l = grpw[:, 0:256].rearrange("p (x r u) -> p x r u", r=2, u=2)
+        g_0 = grpw[:, 256:1280].rearrange("p (x r u) -> p x r u", r=8, u=2)
+        g_1 = grpw[:, 1280:2304].rearrange("p (x r u) -> p x r u", r=8, u=2)
+
+        def w_bank(h, q, eng):
+            pt = psum.tile([P, 512], F32, tag="bank", name="pw%d_%d" % (h, q))
+            for i in range(4):
+                a, u = 2 * q + i // 2, i % 2
+                words = w_sb[:, h, a, :].bitcast(F32)
+                nc.tensor.transpose(pt[:, i * P:(i + 1) * P], words[:, u:256:2], ident[:])
+            copy_out(
+                eng,
+                gww[:, h * 1024:(h + 1) * 1024].rearrange("p (m a u) -> p m a u", a=4, u=2)[:, :, 2 * q:2 * q + 2, :],
+                pt[:].rearrange("p (a u m) -> p m a u", a=2, u=2),
+            )
+
+        def quant_tok(c0, n):
+            nc.vector.quantize_mx(out=tokc[:, c0:c0 + n].bitcast(FP8X4), scales=toks[:, c0:c0 + n], in_=grp[:, 4 * c0:4 * (c0 + n)])
+
+        def quant_w(h):
+            nc.vector.quantize_mx(out=wc[:, half(h)].bitcast(FP8X4), scales=ws[:, half(h)], in_=gw[:, h * 2048:(h + 1) * 2048])
+
+        def mx(t, h):
+            acc = psum.tile([P, 512], F32, tag="bank", name="acc%d_%d" % (t, h))
+            nc.tensor.matmul_mx(
+                out=acc[:],
+                lhsT=tokc[:, t * P:(t + 1) * P].bitcast(FP8X4), lhsT_scale=toks[:, t * P:(t + 1) * P],
+                rhs=wc[:, half(h)].bitcast(FP8X4), rhs_scale=ws[:, half(h)],
+                start=True, stop=True,
+            )
+            accs[(t, h)] = acc
+
+        def group_of(t):
+            return 2 if t == 0 else (t - 1) // 4
+
+        def add_v(t, h):
+            nc.vector.tensor_tensor(out=o_sb[t][:, half(h)], in0=accs[(t, h)][:], in1=posb[group_of(t)][:, half(h)], op=ADD)
+
+        def add_sg(t, h):
+            tmp = keep.tile([P, 512], F32, name="tmp%d_%d" % (t, h))
+            nc.scalar.copy(out=tmp[:], in_=accs[(t, h)][:])
+            nc.gpsimd.tensor_tensor(out=o_sb[t][:, half(h)], in0=tmp[:], in1=posb[group_of(t)][:, half(h)], op=ADD)
+
+        def dram(t, cols):
+            if t == 0:
+                return on[:, 8:10, cols]
+            g, bi = (t - 1) // 4, (t - 1) % 4
+            return ov[bi, :, 10 * g:10 * g + 8, cols]
+
+        def store(t, h=None):
+            cols = slice(0, 1024) if h is None else half(h)
+            nc.sync.dma_start(out=dram(t, cols), in_=o_sb[t][:, cols])
+
+        def load_b():
+            for t in range(2):
+                nc.sync.dma_start(out=v_sb[0:P:2, t, :], in_=vid[t, 2])
+            nc.sync.dma_start(out=pos_sb[1][:], in_=pv[:, 10:18, :])
+
+        regroup(0, 0)
+        regroup(0, 1)
+        load_b()
+        a23 = tok_a(2)
+        copy_out("S", g_l, a23[:, 1])
+        copy_out("S", g_0[:, :, 2:4, :], a23[:, 0])
+        w_bank(0, 0, "S")
+        a01 = tok_a(0)
+        copy_out("V", g_0[:, :, 0:2, :], a01[:, 0])
+        copy_out("V", g_0[:, :, 6:8, :], a01[:, 1])
+        w_bank(0, 1, "V")
+        quant_tok(0, 128)
+        bbc_mm(0)
+        bbc_copy(0)
+        a45 = tok_a(4)
+        copy_out("S", g_0[:, :, 4:6, :], a45[:, 0])
+        pn_mm(0)
+        quant_w(0)
+        copy_out("S", g_1[:, :, 0:2, :], a45[:, 1])
+        make_posb(0, 0)
+        mx(0, 0)
+        quant_tok(128, 512)
+        add_v(0, 0)
+        mx(1, 0)
+        mx(2, 0)
+        store(0, 0)
+        w_bank(1, 0, "S")
+        w_bank(1, 1, "S")
+        add_v(1, 0)
+        store(1, 0)
+        mx(3, 0)
+        mx(4, 0)
+        regroup(1, 0)
+        add_v(2, 0)
+        store(2, 0)
+        bbc_mm(1)
+        bbc_copy(1)
+        make_posb(0, 1)
+        add_v(3, 0)
+        store(3, 0)
+        regroup(1, 1)
+        quant_w(1)
+        b01 = tok_b(0)
+        copy_out("S", g_1[:, :, 2:4, :], b01)
+        b23 = tok_b(2)
+        copy_out("S", g_1[:, :, 4:6, :], b23)
+        b45 = tok_b(4)
+        copy_out("S", g_1[:, :, 6:8, :], b45)
+        pn_mm(1)
+        add_v(4, 0)
+        store(4, 0)
+        mx(1, 1)
+        add_v(1, 1)
+        store(1, 1)
+        mx(2, 1)
+        quant_tok(640, 512)
+        make_posb(1, 0)
+        mx(3, 1)
+        add_sg(2, 1)
+        mx(4, 1)
+        mx(0, 1)
+        add_v(3, 1)
+        store(3, 1)
+        add_v(4, 1)
+        store(4, 1)
+        store(2, 1)
+        add_v(0, 1)
+        store(0, 1)
+        mx(5, 0)
+        mx(6, 0)
+        make_posb(1, 1)
+        mx(7, 0)
+        mx(8, 0)
+        add_v(5, 0)
+        store(5, 0)
+        add_v(6, 0)
+        store(6, 0)
+        mx(5, 1)
+        mx(6, 1)
+        add_sg(7, 0)
+        add_v(8, 0)
+        store(8, 0)
+        mx(7, 1)
+        mx(8, 1)
+        add_sg(6, 1)
+        add_v(5, 1)
+        store(5, 1)
+        store(7, 0)
+        add_v(7, 1)
+        store(7, 1)
+        add_v(8, 1)
+        store(8, 1)
+        store(6, 1)

@@ -17,38 +17,65 @@ def tile_tubeletembedding_kernel(tc, video, W, b, pos_embed, out):
     nc = tc.nc
     with ExitStack() as ctx:
         keep = ctx.enter_context(tc.tile_pool(name="keep", bufs=1))
-        psum = ctx.enter_context(tc.psum_pool(name="psum", bufs=8))
+        psum = ctx.enter_context(tc.psum_pool(name="psum", bufs=4))
+        psum_mx = ctx.enter_context(tc.psum_pool(name="psum_mx", bufs=4))
         ctx.enter_context(tc.manual_schedule())
 
         vid = video.rearrange("b (d t) o (h c y) x -> t c (b d) h (o y x)", t=2, h=2, c=3, y=16)
-        wv = W.rearrange("(h p a) k -> p h a k", h=2, a=4)
+        wv = W.rearrange("(q p a) k -> p q a k", q=4, a=2)
         pv = pos_embed.rearrange("o (s r) e -> (o s) r e", r=18)
         ov = out.rearrange("b (s r) e -> b s r e", r=18)
         on = out.rearrange("b (s r) e -> (b s) r e", r=18)
 
         ident = keep.tile([P, P], F32)
         make_identity(nc, ident[:])
+        zb = keep.tile([P, 1024], BF16)
+        nc.vector.memset(zb[:].bitcast(U32), 0)
         z = keep.tile([P, 1024], BF16)
-        nc.vector.memset(z[:], 0.0)
+        nc.vector.memset(z[:].bitcast(U32), 0)
 
-        v_sb = keep.tile([P, 2, 1536], BF16)
-        w_sb = keep.tile([P, 2, 4, 512], BF16)
+        v_sb = [keep.tile([P, 1536], BF16, name="v%d" % t) for t in range(2)]
+        w_sb = keep.tile([P, 4, 2, 512], BF16)
         pos_sb = [keep.tile([P, 1024], BF16, name="pos%d" % g) for g in range(2)]
-        for t in range(2):
+
+        def load_a(t):
             for c in range(2):
-                nc.sync.dma_start(out=v_sb[c:P:2, t, :], in_=vid[t, c])
-        nc.sync.dma_start(out=w_sb[:, 0, 0:2, :], in_=wv[:, 0, 0:2, :])
-        nc.sync.dma_start(out=w_sb[:, 0, 2:4, :], in_=wv[:, 0, 2:4, :])
-        nc.sync.dma_start(out=z[32:33, :], in_=b.unsqueeze(0))
-        nc.sync.dma_start(out=z[0:32, :], in_=pv[:, 8:10, :])
-        nc.sync.dma_start(out=pos_sb[0][:], in_=pv[:, 0:8, :])
-        nc.sync.dma_start(out=w_sb[:, 1, :, :], in_=wv[:, 1, :, :])
+                nc.sync.dma_start(out=v_sb[t][c:P:2, :], in_=vid[t, c])
+
+        def load_b():
+            for t in range(2):
+                nc.sync.dma_start(out=v_sb[t][0:P:2, :], in_=vid[t, 2])
+
+        def load_w(q0, q1):
+            nc.sync.dma_start(out=w_sb[:, q0:q1], in_=wv[:, q0:q1])
+
+        def load_zb():
+            nc.sync.dma_start(out=zb[0:1, :], in_=b.unsqueeze(0))
+
+        def load_z():
+            nc.sync.dma_start(out=z[0:32, :], in_=pv[:, 8:10, :])
+            nc.sync.dma_start(out=z[32:33, :], in_=b.unsqueeze(0))
+
+        def load_pos(g):
+            nc.sync.dma_start(out=pos_sb[g][:], in_=pv[:, 10 * g:10 * g + 8, :])
+
+        load_a(0)
+        load_zb()
+        load_a(1)
+        load_w(0, 1)
+        load_w(1, 2)
+        load_z()
+        load_pos(0)
+        load_pos(1)
+        load_w(2, 4)
 
         perm = keep.tile([P, P], F32)
         nc.vector.tensor_copy(
             out=perm[:].rearrange("p (c x) -> p c x", c=2),
             in_=ident[:].rearrange("p (x c) -> p c x", c=2),
         )
+        sel_b = keep.tile([P, P], BF16)
+        nc.vector.tensor_copy(out=sel_b[:], in_=ident[:, 0:1].to_broadcast([P, P]))
         sel_n = keep.tile([P, P], BF16)
         nc.vector.tensor_tensor(
             out=sel_n[:].rearrange("p (c q) -> p c q", c=4),
@@ -56,8 +83,8 @@ def tile_tubeletembedding_kernel(tc, video, W, b, pos_embed, out):
             in1=ident[:, 32:33].unsqueeze(1).to_broadcast([P, 4, 32]),
             op=ADD,
         )
-        sel_b = keep.tile([P, P], BF16)
-        nc.vector.tensor_copy(out=sel_b[:], in_=ident[:, 32:33].to_broadcast([P, P]))
+        ident_h = keep.tile([P, P], BF16)
+        nc.vector.tensor_copy(out=ident_h[:], in_=ident[:])
 
         v2 = [keep.tile([P, 3072], BF16, name="v2_%d" % s) for s in range(2)]
         grp = keep.tile([P, 4608], BF16, align_bytes=64)
@@ -71,7 +98,6 @@ def tile_tubeletembedding_kernel(tc, video, W, b, pos_embed, out):
         posb = [keep.tile([P, 1024], F32, name="posb%d" % g) for g in range(3)]
         o_sb = [keep.tile([P, 1024], F32, name="o%d" % t) for t in range(9)]
         bbcs = keep.tile([P, 1024], F32)
-        bbc = {}
         accs = {}
 
         def half(h):
@@ -83,26 +109,42 @@ def tile_tubeletembedding_kernel(tc, video, W, b, pos_embed, out):
             else:
                 nc.scalar.copy(out=dst, in_=src)
 
-        def bbc_mm(h):
-            bbc[h] = psum.tile([P, 512], F32, tag="bank", name="bbc%d" % h)
-            nc.tensor.matmul(out=bbc[h][:], lhsT=sel_b[:], rhs=z[:, half(h)], start=True, stop=True)
+        def warm(n):
+            pw = psum.tile([P, 512], F32, tag="bank", name="warm")
+            for i in range(n):
+                nc.tensor.matmul(out=pw[:, i * P:(i + 1) * P], lhsT=ident[:], rhs=ident[:], start=True, stop=True)
+
+        def bbc_make(h):
+            pb = psum.tile([P, 512], F32, tag="bank", name="bbc%d" % h)
+            nc.tensor.matmul(out=pb[:], lhsT=sel_b[:], rhs=zb[:, half(h)], start=True, stop=True)
+            nc.scalar.copy(out=bbcs[:, half(h)], in_=pb[:])
+
+        pns = {}
 
         def pn_mm(h):
-            pn = psum.tile([P, 512], F32, tag="bank", name="pn%d" % h)
-            nc.tensor.matmul(out=pn[:], lhsT=sel_n[:], rhs=z[:, half(h)], start=True, stop=True)
-            nc.scalar.copy(out=posb[2][:, half(h)], in_=pn[:])
+            pns[h] = psum.tile([P, 512], F32, tag="bank", name="pn%d" % h)
+            nc.tensor.matmul(out=pns[h][:], lhsT=sel_n[:], rhs=z[:, half(h)], start=True, stop=True)
 
-        def bbc_copy(h):
-            nc.scalar.copy(out=bbcs[:, half(h)], in_=bbc[h][:])
+        def pn_copy(h):
+            nc.scalar.copy(out=posb[2][:, half(h)], in_=pns[h][:])
 
-        def make_posb(g, h):
+        def posb_g(g, h):
             nc.gpsimd.tensor_tensor(out=posb[g][:, half(h)], in0=pos_sb[g][:, half(h)], in1=bbcs[:, half(h)], op=ADD)
 
-        def regroup(s, t):
+        def posb_v(g, h):
+            nc.vector.tensor_tensor(out=posb[g][:, half(h)], in0=pos_sb[g][:, half(h)], in1=bbcs[:, half(h)], op=ADD)
+
+        def posb_pe(g, h):
+            pb = psum.tile([P, 512], F32, tag="bank", name="pp%d_%d" % (g, h))
+            nc.tensor.matmul(out=pb[:], lhsT=ident_h[:], rhs=pos_sb[g][:, half(h)], start=True, stop=False)
+            nc.tensor.matmul(out=pb[:], lhsT=sel_b[:], rhs=zb[:, half(h)], start=False, stop=True)
+            nc.scalar.copy(out=posb[g][:, half(h)], in_=pb[:])
+
+        def regroup(s, t, eng="V"):
             dst = v2[s][:].bitcast(F32).rearrange("p (j u t y x) -> p t j u y x", j=6, u=2, t=2, y=16)
-            src = v_sb[:, t, :].bitcast(F32).rearrange("p (y j x u) -> p j u y x", y=16, j=6, u=2)
+            src = v_sb[t][:].bitcast(F32).rearrange("p (y j x u) -> p j u y x", y=16, j=6, u=2)
             for u in range(2):
-                nc.vector.tensor_copy(out=dst[:, t, :, u], in_=src[:, :, u])
+                copy_out(eng, dst[:, t, :, u], src[:, :, u])
 
         def tok_a(j0):
             pt = psum.tile([P, 512], F32, tag="bank", name="pa%d" % j0)
@@ -124,26 +166,30 @@ def tile_tubeletembedding_kernel(tc, video, W, b, pos_embed, out):
         g_0 = grpw[:, 256:1280].rearrange("p (x r u) -> p x r u", r=8, u=2)
         g_1 = grpw[:, 1280:2304].rearrange("p (x r u) -> p x r u", r=8, u=2)
 
-        def w_bank(h, q, eng):
-            pt = psum.tile([P, 512], F32, tag="bank", name="pw%d_%d" % (h, q))
+        pws = {}
+
+        def w_t(q):
+            pws[q] = psum.tile([P, 512], F32, tag="bank", name="pw%d" % q)
             for i in range(4):
-                a, u = 2 * q + i // 2, i % 2
-                words = w_sb[:, h, a, :].bitcast(F32)
-                nc.tensor.transpose(pt[:, i * P:(i + 1) * P], words[:, u:256:2], ident[:])
+                a, u = i // 2, i % 2
+                words = w_sb[:, q, a, :].bitcast(F32)
+                nc.tensor.transpose(pws[q][:, i * P:(i + 1) * P], words[:, u:256:2], ident[:])
+
+        def w_c(q, eng):
             copy_out(
                 eng,
-                gww[:, h * 1024:(h + 1) * 1024].rearrange("p (m a u) -> p m a u", a=4, u=2)[:, :, 2 * q:2 * q + 2, :],
-                pt[:].rearrange("p (a u m) -> p m a u", a=2, u=2),
+                gww[:, q * 512:(q + 1) * 512].rearrange("p (m a u) -> p m a u", a=2, u=2),
+                pws[q][:].rearrange("p (a u m) -> p m a u", a=2, u=2),
             )
 
         def quant_tok(c0, n):
             nc.vector.quantize_mx(out=tokc[:, c0:c0 + n].bitcast(FP8X4), scales=toks[:, c0:c0 + n], in_=grp[:, 4 * c0:4 * (c0 + n)])
 
-        def quant_w(h):
-            nc.vector.quantize_mx(out=wc[:, half(h)].bitcast(FP8X4), scales=ws[:, half(h)], in_=gw[:, h * 2048:(h + 1) * 2048])
+        def quant_w(c0, n):
+            nc.vector.quantize_mx(out=wc[:, c0:c0 + n].bitcast(FP8X4), scales=ws[:, c0:c0 + n], in_=gw[:, 4 * c0:4 * (c0 + n)])
 
         def mx(t, h):
-            acc = psum.tile([P, 512], F32, tag="bank", name="acc%d_%d" % (t, h))
+            acc = psum_mx.tile([P, 512], F32, tag="acc", name="acc%d_%d" % (t, h))
             nc.tensor.matmul_mx(
                 out=acc[:],
                 lhsT=tokc[:, t * P:(t + 1) * P].bitcast(FP8X4), lhsT_scale=toks[:, t * P:(t + 1) * P],
@@ -173,101 +219,102 @@ def tile_tubeletembedding_kernel(tc, video, W, b, pos_embed, out):
             cols = slice(0, 1024) if h is None else half(h)
             nc.sync.dma_start(out=dram(t, cols), in_=o_sb[t][:, cols])
 
-        def load_b():
-            for t in range(2):
-                nc.sync.dma_start(out=v_sb[0:P:2, t, :], in_=vid[t, 2])
-            nc.sync.dma_start(out=pos_sb[1][:], in_=pv[:, 10:18, :])
-
+        warm(4)
+        bbc_make(0)
+        bbc_make(1)
+        posb_g(0, 0)
+        posb_g(0, 1)
+        posb_g(1, 0)
         regroup(0, 0)
         regroup(0, 1)
         load_b()
+        w_t(0)
         a23 = tok_a(2)
-        copy_out("S", g_l, a23[:, 1])
-        copy_out("S", g_0[:, :, 2:4, :], a23[:, 0])
-        w_bank(0, 0, "S")
-        a01 = tok_a(0)
-        copy_out("V", g_0[:, :, 0:2, :], a01[:, 0])
-        copy_out("V", g_0[:, :, 6:8, :], a01[:, 1])
-        w_bank(0, 1, "V")
+        w_c(0, "S")
+        copy_out("V", g_l, a23[:, 1])
+        copy_out("V", g_0[:, :, 2:4, :], a23[:, 0])
+        w_t(1)
         quant_tok(0, 128)
-        bbc_mm(0)
-        bbc_copy(0)
+        w_c(1, "S")
+        quant_w(0, 256)
+        a01 = tok_a(0)
+        copy_out("S", g_0[:, :, 0:2, :], a01[:, 0])
+        copy_out("S", g_0[:, :, 6:8, :], a01[:, 1])
+        quant_w(256, 256)
         a45 = tok_a(4)
-        copy_out("S", g_0[:, :, 4:6, :], a45[:, 0])
+        copy_out("V", g_0[:, :, 4:6, :], a45[:, 0])
         pn_mm(0)
-        quant_w(0)
-        copy_out("S", g_1[:, :, 0:2, :], a45[:, 1])
-        make_posb(0, 0)
+        pn_copy(0)
         mx(0, 0)
         quant_tok(128, 512)
+        w_t(2)
+        w_t(3)
+        w_c(2, "S")
+        w_c(3, "S")
+        copy_out("V", g_1[:, :, 0:2, :], a45[:, 1])
         add_v(0, 0)
+        store(0, 0)
         mx(1, 0)
         mx(2, 0)
-        store(0, 0)
-        w_bank(1, 0, "S")
-        w_bank(1, 1, "S")
+        mx(3, 0)
         add_v(1, 0)
         store(1, 0)
-        mx(3, 0)
-        mx(4, 0)
-        regroup(1, 0)
-        add_v(2, 0)
-        store(2, 0)
-        bbc_mm(1)
-        bbc_copy(1)
-        make_posb(0, 1)
+        add_sg(2, 0)
+        quant_w(512, 512)
+        regroup(1, 1, "S")
         add_v(3, 0)
         store(3, 0)
-        regroup(1, 1)
-        quant_w(1)
-        b01 = tok_b(0)
-        copy_out("S", g_1[:, :, 2:4, :], b01)
-        b23 = tok_b(2)
-        copy_out("S", g_1[:, :, 4:6, :], b23)
-        b45 = tok_b(4)
-        copy_out("S", g_1[:, :, 6:8, :], b45)
-        pn_mm(1)
+        mx(4, 0)
+        regroup(1, 0)
+        mx(1, 1)
+        mx(2, 1)
+        mx(3, 1)
         add_v(4, 0)
         store(4, 0)
-        mx(1, 1)
+        store(2, 0)
+        add_sg(2, 1)
+        b01 = tok_b(0)
+        b23 = tok_b(2)
+        b45 = tok_b(4)
         add_v(1, 1)
         store(1, 1)
-        mx(2, 1)
-        quant_tok(640, 512)
-        make_posb(1, 0)
-        mx(3, 1)
-        add_sg(2, 1)
-        mx(4, 1)
-        mx(0, 1)
+        copy_out("S", g_1[:, :, 2:4, :], b01)
+        copy_out("S", g_1[:, :, 4:6, :], b23)
+        copy_out("S", g_1[:, :, 6:8, :], b45)
         add_v(3, 1)
         store(3, 1)
-        add_v(4, 1)
-        store(4, 1)
+        mx(4, 1)
+        pn_mm(1)
+        mx(0, 1)
+        quant_tok(640, 512)
+        add_sg(4, 1)
         store(2, 1)
-        add_v(0, 1)
-        store(0, 1)
+        pn_copy(1)
+        posb_v(1, 1)
+        add_sg(0, 1)
         mx(5, 0)
         mx(6, 0)
-        make_posb(1, 1)
         mx(7, 0)
-        mx(8, 0)
+        store(4, 1)
         add_v(5, 0)
         store(5, 0)
-        add_v(6, 0)
-        store(6, 0)
+        add_sg(6, 0)
+        mx(8, 0)
         mx(5, 1)
+        add_v(7, 0)
+        store(7, 0)
+        store(0, 1)
         mx(6, 1)
-        add_sg(7, 0)
+        add_sg(6, 1)
         add_v(8, 0)
         store(8, 0)
         mx(7, 1)
         mx(8, 1)
-        add_sg(6, 1)
         add_v(5, 1)
         store(5, 1)
-        store(7, 0)
+        store(6, 0)
         add_v(7, 1)
         store(7, 1)
         add_v(8, 1)
-        store(8, 1)
         store(6, 1)
+        store(8, 1)

@@ -17,8 +17,7 @@ def tile_tubeletembedding_kernel(tc, video, W, b, pos_embed, out):
     nc = tc.nc
     with ExitStack() as ctx:
         keep = ctx.enter_context(tc.tile_pool(name="keep", bufs=1))
-        psum = ctx.enter_context(tc.psum_pool(name="psum", bufs=4))
-        psum_mx = ctx.enter_context(tc.psum_pool(name="psum_mx", bufs=4))
+        psum = ctx.enter_context(tc.psum_pool(name="psum", bufs=1))
         ctx.enter_context(tc.manual_schedule())
 
         vid = video.rearrange("b (d t) o (h c y) x -> t c (b d) h (o y x)", t=2, h=2, c=3, y=16)
@@ -99,6 +98,14 @@ def tile_tubeletembedding_kernel(tc, video, W, b, pos_embed, out):
         o_sb = [keep.tile([P, 1024], F32, name="o%d" % t) for t in range(9)]
         bbcs = keep.tile([P, 1024], F32)
         accs = {}
+        turn = {"t": 0, "acc": 0}
+        banks = {"t": 4, "acc": 4}
+
+        def bank(kind, name):
+            i = turn[kind] % banks[kind]
+            turn[kind] = turn[kind] + 1
+            return psum.tile([P, 512], F32, tag="%s%d" % (kind, i), name=name)
+
 
         def half(h):
             return slice(h * 512, (h + 1) * 512)
@@ -110,19 +117,19 @@ def tile_tubeletembedding_kernel(tc, video, W, b, pos_embed, out):
                 nc.scalar.copy(out=dst, in_=src)
 
         def warm(n):
-            pw = psum.tile([P, 512], F32, tag="bank", name="warm")
+            pw = bank("t", "warm")
             for i in range(n):
                 nc.tensor.matmul(out=pw[:, i * P:(i + 1) * P], lhsT=ident[:], rhs=ident[:], start=True, stop=True)
 
         def bbc_make(h):
-            pb = psum.tile([P, 512], F32, tag="bank", name="bbc%d" % h)
+            pb = bank("t", "bbc%d" % h)
             nc.tensor.matmul(out=pb[:], lhsT=sel_b[:], rhs=zb[:, half(h)], start=True, stop=True)
             nc.scalar.copy(out=bbcs[:, half(h)], in_=pb[:])
 
         pns = {}
 
         def pn_mm(h):
-            pns[h] = psum.tile([P, 512], F32, tag="bank", name="pn%d" % h)
+            pns[h] = bank("t", "pn%d" % h)
             nc.tensor.matmul(out=pns[h][:], lhsT=sel_n[:], rhs=z[:, half(h)], start=True, stop=True)
 
         def pn_copy(h):
@@ -135,7 +142,7 @@ def tile_tubeletembedding_kernel(tc, video, W, b, pos_embed, out):
             nc.vector.tensor_tensor(out=posb[g][:, half(h)], in0=pos_sb[g][:, half(h)], in1=bbcs[:, half(h)], op=ADD)
 
         def posb_pe(g, h):
-            pb = psum.tile([P, 512], F32, tag="bank", name="pp%d_%d" % (g, h))
+            pb = bank("t", "pp%d_%d" % (g, h))
             nc.tensor.matmul(out=pb[:], lhsT=ident_h[:], rhs=pos_sb[g][:, half(h)], start=True, stop=False)
             nc.tensor.matmul(out=pb[:], lhsT=sel_b[:], rhs=zb[:, half(h)], start=False, stop=True)
             nc.scalar.copy(out=posb[g][:, half(h)], in_=pb[:])
@@ -147,7 +154,7 @@ def tile_tubeletembedding_kernel(tc, video, W, b, pos_embed, out):
                 copy_out(eng, dst[:, t, :, u], src[:, :, u])
 
         def tok_a(j0):
-            pt = psum.tile([P, 512], F32, tag="bank", name="pa%d" % j0)
+            pt = bank("t", "pa%d" % j0)
             vw = v2[0][:].bitcast(F32)
             for i in range(4):
                 r = 2 * j0 + i
@@ -155,7 +162,7 @@ def tile_tubeletembedding_kernel(tc, video, W, b, pos_embed, out):
             return pt[:].rearrange("p (j u c x) -> p c x j u", j=2, u=2, c=2)
 
         def tok_b(j0):
-            pt = psum.tile([P, 512], F32, tag="bank", name="pb%d" % j0)
+            pt = bank("t", "pb%d" % j0)
             vw = v2[1][:].bitcast(F32)
             for i in range(4):
                 r = 2 * j0 + i
@@ -169,7 +176,7 @@ def tile_tubeletembedding_kernel(tc, video, W, b, pos_embed, out):
         pws = {}
 
         def w_t(q):
-            pws[q] = psum.tile([P, 512], F32, tag="bank", name="pw%d" % q)
+            pws[q] = bank("t", "pw%d" % q)
             for i in range(4):
                 a, u = i // 2, i % 2
                 words = w_sb[:, q, a, :].bitcast(F32)
@@ -189,7 +196,7 @@ def tile_tubeletembedding_kernel(tc, video, W, b, pos_embed, out):
             nc.vector.quantize_mx(out=wc[:, c0:c0 + n].bitcast(FP8X4), scales=ws[:, c0:c0 + n], in_=gw[:, 4 * c0:4 * (c0 + n)])
 
         def mx(t, h):
-            acc = psum_mx.tile([P, 512], F32, tag="acc", name="acc%d_%d" % (t, h))
+            acc = bank("acc", "acc%d_%d" % (t, h))
             nc.tensor.matmul_mx(
                 out=acc[:],
                 lhsT=tokc[:, t * P:(t + 1) * P].bitcast(FP8X4), lhsT_scale=toks[:, t * P:(t + 1) * P],

@@ -28,8 +28,6 @@ def tile_tubeletembedding_kernel(tc, video, W, b, pos_embed, out):
 
         ident = keep.tile([P, P], F32)
         make_identity(nc, ident[:])
-        zb = keep.tile([P, 1024], BF16)
-        nc.vector.memset(zb[:].bitcast(U32), 0)
         z = keep.tile([P, 1024], BF16)
         nc.vector.memset(z[:].bitcast(U32), 0)
 
@@ -48,24 +46,19 @@ def tile_tubeletembedding_kernel(tc, video, W, b, pos_embed, out):
         def load_w(q0, q1):
             nc.sync.dma_start(out=w_sb[:, q0:q1], in_=wv[:, q0:q1])
 
-        def load_zb():
-            nc.sync.dma_start(out=zb[0:1, :], in_=b.unsqueeze(0))
-
         def load_z():
-            nc.sync.dma_start(out=z[0:32, :], in_=pv[:, 8:10, :])
             nc.sync.dma_start(out=z[32:33, :], in_=b.unsqueeze(0))
+            nc.sync.dma_start(out=z[0:32, :], in_=pv[:, 8:10, :])
 
         def load_pos(g):
             nc.sync.dma_start(out=pos_sb[g][:], in_=pv[:, 10 * g:10 * g + 8, :])
 
         load_a(0)
-        load_zb()
         load_a(1)
         load_w(0, 1)
         load_w(1, 2)
         load_z()
         load_pos(0)
-        load_pos(1)
         load_w(2, 4)
 
         perm = keep.tile([P, P], F32)
@@ -74,7 +67,7 @@ def tile_tubeletembedding_kernel(tc, video, W, b, pos_embed, out):
             in_=ident[:].rearrange("p (x c) -> p c x", c=2),
         )
         sel_b = keep.tile([P, P], BF16)
-        nc.vector.tensor_copy(out=sel_b[:], in_=ident[:, 0:1].to_broadcast([P, P]))
+        nc.vector.tensor_copy(out=sel_b[:], in_=ident[:, 32:33].to_broadcast([P, P]))
         sel_n = keep.tile([P, P], BF16)
         nc.vector.tensor_tensor(
             out=sel_n[:].rearrange("p (c q) -> p c q", c=4),
@@ -99,7 +92,7 @@ def tile_tubeletembedding_kernel(tc, video, W, b, pos_embed, out):
         bbcs = keep.tile([P, 1024], F32)
         accs = {}
         turn = {"t": 0, "acc": 0}
-        banks = {"t": 4, "acc": 4}
+        banks = {"t": 5, "acc": 3}
 
         def bank(kind, name):
             i = turn[kind] % banks[kind]
@@ -121,10 +114,14 @@ def tile_tubeletembedding_kernel(tc, video, W, b, pos_embed, out):
             for i in range(n):
                 nc.tensor.matmul(out=pw[:, i * P:(i + 1) * P], lhsT=ident[:], rhs=ident[:], start=True, stop=True)
 
-        def bbc_make(h):
-            pb = bank("t", "bbc%d" % h)
-            nc.tensor.matmul(out=pb[:], lhsT=sel_b[:], rhs=zb[:, half(h)], start=True, stop=True)
-            nc.scalar.copy(out=bbcs[:, half(h)], in_=pb[:])
+        bbc = {}
+
+        def bbc_mm(h, kind="t"):
+            bbc[h] = bank(kind, "bbc%d" % h)
+            nc.tensor.matmul(out=bbc[h][:], lhsT=sel_b[:], rhs=z[:, half(h)], start=True, stop=True)
+
+        def bbc_copy(h, eng):
+            copy_out(eng, bbcs[:, half(h)], bbc[h][:])
 
         pns = {}
 
@@ -139,19 +136,27 @@ def tile_tubeletembedding_kernel(tc, video, W, b, pos_embed, out):
             nc.gpsimd.tensor_tensor(out=posb[g][:, half(h)], in0=pos_sb[g][:, half(h)], in1=bbcs[:, half(h)], op=ADD)
 
         def posb_v(g, h):
-            nc.vector.tensor_tensor(out=posb[g][:, half(h)], in0=pos_sb[g][:, half(h)], in1=bbcs[:, half(h)], op=ADD)
+            nc.vector.tensor_tensor(out=posb[g][:, half(h)], in0=bbc[h][:], in1=pos_sb[g][:, half(h)], op=ADD)
 
-        def posb_pe(g, h):
-            pb = bank("t", "pp%d_%d" % (g, h))
-            nc.tensor.matmul(out=pb[:], lhsT=ident_h[:], rhs=pos_sb[g][:, half(h)], start=True, stop=False)
-            nc.tensor.matmul(out=pb[:], lhsT=sel_b[:], rhs=zb[:, half(h)], start=False, stop=True)
-            nc.scalar.copy(out=posb[g][:, half(h)], in_=pb[:])
+        pps = {}
+
+        def pp_mm(g, h):
+            pps[(g, h)] = bank("t", "pp%d_%d" % (g, h))
+            nc.tensor.matmul(out=pps[(g, h)][:], lhsT=ident_h[:], rhs=pos_sb[g][:, half(h)], start=True, stop=False)
+            nc.tensor.matmul(out=pps[(g, h)][:], lhsT=sel_b[:], rhs=z[:, half(h)], start=False, stop=True)
+
+        def pp_copy(g, h):
+            nc.scalar.copy(out=posb[g][:, half(h)], in_=pps[(g, h)][:])
 
         def regroup(s, t, eng="V"):
             dst = v2[s][:].bitcast(F32).rearrange("p (j u t y x) -> p t j u y x", j=6, u=2, t=2, y=16)
             src = v_sb[t][:].bitcast(F32).rearrange("p (y j x u) -> p j u y x", y=16, j=6, u=2)
-            for u in range(2):
-                copy_out(eng, dst[:, t, :, u], src[:, :, u])
+            if eng == "S2":
+                copy_out("V", dst[:, t, :, 0], src[:, :, 0])
+                copy_out("S", dst[:, t, :, 1], src[:, :, 1])
+            else:
+                for u in range(2):
+                    copy_out(eng, dst[:, t, :, u], src[:, :, u])
 
         def tok_a(j0):
             pt = bank("t", "pa%d" % j0)
@@ -227,99 +232,102 @@ def tile_tubeletembedding_kernel(tc, video, W, b, pos_embed, out):
             nc.sync.dma_start(out=dram(t, cols), in_=o_sb[t][:, cols])
 
         warm(4)
-        bbc_make(0)
-        bbc_make(1)
-        posb_g(0, 0)
-        posb_g(0, 1)
-        posb_g(1, 0)
         regroup(0, 0)
         regroup(0, 1)
         load_b()
+        load_pos(1)
         w_t(0)
-        a23 = tok_a(2)
         w_c(0, "S")
+        a23 = tok_a(2)
         copy_out("V", g_l, a23[:, 1])
         copy_out("V", g_0[:, :, 2:4, :], a23[:, 0])
         w_t(1)
-        quant_tok(0, 128)
         w_c(1, "S")
-        quant_w(0, 256)
         a01 = tok_a(0)
+        quant_tok(0, 128)
         copy_out("S", g_0[:, :, 0:2, :], a01[:, 0])
         copy_out("S", g_0[:, :, 6:8, :], a01[:, 1])
-        quant_w(256, 256)
         a45 = tok_a(4)
+        quant_w(0, 256)
         copy_out("V", g_0[:, :, 4:6, :], a45[:, 0])
+        quant_w(256, 256)
         pn_mm(0)
         pn_copy(0)
-        mx(0, 0)
-        quant_tok(128, 512)
+        bbc_mm(0)
         w_t(2)
-        w_t(3)
         w_c(2, "S")
-        w_c(3, "S")
+        mx(0, 0)
+        w_t(3)
+        quant_tok(128, 512)
+        add_sg(0, 0)
+        posb_v(0, 0)
         copy_out("V", g_1[:, :, 0:2, :], a45[:, 1])
-        add_v(0, 0)
-        store(0, 0)
+        w_c(3, "S")
         mx(1, 0)
         mx(2, 0)
         mx(3, 0)
+        bbc_mm(1)
         add_v(1, 0)
         store(1, 0)
-        add_sg(2, 0)
+        add_sg(3, 0)
+        add_v(2, 0)
+        store(2, 0)
+        store(0, 0)
         quant_w(512, 512)
-        regroup(1, 1, "S")
-        add_v(3, 0)
-        store(3, 0)
         mx(4, 0)
-        regroup(1, 0)
+        regroup(1, 0, "S")
+        posb_v(0, 1)
         mx(1, 1)
         mx(2, 1)
-        mx(3, 1)
+        mx(0, 1)
         add_v(4, 0)
         store(4, 0)
-        store(2, 0)
-        add_sg(2, 1)
+        regroup(1, 1, "S2")
+        pn_mm(1)
+        pn_copy(1)
+        add_sg(0, 1)
+        store(3, 0)
+        add_v(1, 1)
+        store(1, 1)
+        bbc_mm(0)
+        bbc_mm(1)
         b01 = tok_b(0)
         b23 = tok_b(2)
         b45 = tok_b(4)
-        add_v(1, 1)
-        store(1, 1)
+        mx(3, 1)
+        mx(4, 1)
+        add_v(2, 1)
+        store(2, 1)
         copy_out("S", g_1[:, :, 2:4, :], b01)
         copy_out("S", g_1[:, :, 4:6, :], b23)
         copy_out("S", g_1[:, :, 6:8, :], b45)
-        add_v(3, 1)
-        store(3, 1)
-        mx(4, 1)
-        pn_mm(1)
-        mx(0, 1)
-        quant_tok(640, 512)
+        posb_v(1, 0)
+        store(0, 1)
         add_sg(4, 1)
-        store(2, 1)
-        pn_copy(1)
+        quant_tok(640, 512)
         posb_v(1, 1)
-        add_sg(0, 1)
         mx(5, 0)
         mx(6, 0)
         mx(7, 0)
-        store(4, 1)
+        add_v(3, 1)
+        store(3, 1)
+        add_sg(6, 0)
         add_v(5, 0)
         store(5, 0)
-        add_sg(6, 0)
+        store(4, 1)
         mx(8, 0)
         mx(5, 1)
         add_v(7, 0)
         store(7, 0)
-        store(0, 1)
         mx(6, 1)
-        add_sg(6, 1)
-        add_v(8, 0)
-        store(8, 0)
+        add_sg(8, 0)
+        store(6, 0)
         mx(7, 1)
         mx(8, 1)
         add_v(5, 1)
         store(5, 1)
-        store(6, 0)
+        add_sg(6, 1)
+        store(8, 0)
         add_v(7, 1)
         store(7, 1)
         add_v(8, 1)

@@ -28,6 +28,8 @@ def tile_tubeletembedding_kernel(tc, video, W, b, pos_embed, out):
 
         ident = keep.tile([P, P], F32)
         make_identity(nc, ident[:])
+        b8 = keep.tile([P, P], BF16)
+        nc.vector.memset(b8[:].bitcast(U32), 0)
         z = keep.tile([P, 1024], BF16)
         nc.vector.memset(z[:].bitcast(U32), 0)
 
@@ -50,16 +52,21 @@ def tile_tubeletembedding_kernel(tc, video, W, b, pos_embed, out):
             nc.sync.dma_start(out=z[32:33, :], in_=b.unsqueeze(0))
             nc.sync.dma_start(out=z[0:32, :], in_=pv[:, 8:10, :])
 
-        def load_pos(g):
-            nc.sync.dma_start(out=pos_sb[g][:], in_=pv[:, 10 * g:10 * g + 8, :])
+        def load_b8():
+            nc.sync.dma_start(out=b8[0:8, :], in_=b.rearrange("(m e) -> m e", m=8))
+
+        def load_pos(g, h=None):
+            cols = slice(0, 1024) if h is None else slice(h * 512, (h + 1) * 512)
+            nc.sync.dma_start(out=pos_sb[g][:, cols], in_=pv[:, 10 * g:10 * g + 8, cols])
 
         load_a(0)
+        load_b8()
         load_a(1)
         load_w(0, 1)
+        load_pos(0, 0)
         load_w(1, 2)
         load_z()
-        load_pos(0)
-        load_w(2, 4)
+        load_pos(0, 1)
 
         perm = keep.tile([P, P], F32)
         nc.vector.tensor_copy(
@@ -91,13 +98,11 @@ def tile_tubeletembedding_kernel(tc, video, W, b, pos_embed, out):
         o_sb = [keep.tile([P, 1024], F32, name="o%d" % t) for t in range(9)]
         bbcs = keep.tile([P, 1024], F32)
         accs = {}
-        turn = {"t": 0, "acc": 0}
-        banks = {"t": 5, "acc": 3}
+        order = []
 
-        def bank(kind, name):
-            i = turn[kind] % banks[kind]
-            turn[kind] = turn[kind] + 1
-            return psum.tile([P, 512], F32, tag="%s%d" % (kind, i), name=name)
+        def bank(name):
+            order.append(name)
+            return psum.tile([P, 512], F32, tag="bank%d" % (len(order) % 7), name=name)
 
 
         def half(h):
@@ -110,23 +115,27 @@ def tile_tubeletembedding_kernel(tc, video, W, b, pos_embed, out):
                 nc.scalar.copy(out=dst, in_=src)
 
         def warm(n):
-            pw = bank("t", "warm")
+            pw = bank("warm")
             for i in range(n):
                 nc.tensor.matmul(out=pw[:, i * P:(i + 1) * P], lhsT=ident[:], rhs=ident[:], start=True, stop=True)
 
-        bbc = {}
+        bt = keep.tile([P, 8], BF16)
+        bbt = psum.tile([P, 1024], BF16, tag="bbt")
 
-        def bbc_mm(h, kind="t"):
-            bbc[h] = bank(kind, "bbc%d" % h)
-            nc.tensor.matmul(out=bbc[h][:], lhsT=sel_b[:], rhs=z[:, half(h)], start=True, stop=True)
+        def bias_columns():
+            pt = bank("pbt")
+            ph = pt[:].bitcast(BF16)
+            nc.tensor.transpose(ph[:, 0:P], b8[:], ident_h[:])
+            nc.scalar.copy(out=bt[:], in_=ph[:, 0:8])
 
-        def bbc_copy(h, eng):
-            copy_out(eng, bbcs[:, half(h)], bbc[h][:])
+        def bias_spread(h):
+            for m in range(4 * h, 4 * h + 4):
+                nc.tensor.transpose(bbt[:, m * P:(m + 1) * P], bt[:, m:m + 1].to_broadcast([P, P]), ident_h[:])
 
         pns = {}
 
         def pn_mm(h):
-            pns[h] = bank("t", "pn%d" % h)
+            pns[h] = bank("pn%d" % h)
             nc.tensor.matmul(out=pns[h][:], lhsT=sel_n[:], rhs=z[:, half(h)], start=True, stop=True)
 
         def pn_copy(h):
@@ -136,12 +145,12 @@ def tile_tubeletembedding_kernel(tc, video, W, b, pos_embed, out):
             nc.gpsimd.tensor_tensor(out=posb[g][:, half(h)], in0=pos_sb[g][:, half(h)], in1=bbcs[:, half(h)], op=ADD)
 
         def posb_v(g, h):
-            nc.vector.tensor_tensor(out=posb[g][:, half(h)], in0=bbc[h][:], in1=pos_sb[g][:, half(h)], op=ADD)
+            nc.vector.tensor_tensor(out=posb[g][:, half(h)], in0=bbt[:, half(h)], in1=pos_sb[g][:, half(h)], op=ADD)
 
         pps = {}
 
         def pp_mm(g, h):
-            pps[(g, h)] = bank("t", "pp%d_%d" % (g, h))
+            pps[(g, h)] = bank("pp%d_%d" % (g, h))
             nc.tensor.matmul(out=pps[(g, h)][:], lhsT=ident_h[:], rhs=pos_sb[g][:, half(h)], start=True, stop=False)
             nc.tensor.matmul(out=pps[(g, h)][:], lhsT=sel_b[:], rhs=z[:, half(h)], start=False, stop=True)
 
@@ -159,7 +168,7 @@ def tile_tubeletembedding_kernel(tc, video, W, b, pos_embed, out):
                     copy_out(eng, dst[:, t, :, u], src[:, :, u])
 
         def tok_a(j0):
-            pt = bank("t", "pa%d" % j0)
+            pt = bank("pa%d" % j0)
             vw = v2[0][:].bitcast(F32)
             for i in range(4):
                 r = 2 * j0 + i
@@ -167,7 +176,7 @@ def tile_tubeletembedding_kernel(tc, video, W, b, pos_embed, out):
             return pt[:].rearrange("p (j u c x) -> p c x j u", j=2, u=2, c=2)
 
         def tok_b(j0):
-            pt = bank("t", "pb%d" % j0)
+            pt = bank("pb%d" % j0)
             vw = v2[1][:].bitcast(F32)
             for i in range(4):
                 r = 2 * j0 + i
@@ -181,7 +190,7 @@ def tile_tubeletembedding_kernel(tc, video, W, b, pos_embed, out):
         pws = {}
 
         def w_t(q):
-            pws[q] = bank("t", "pw%d" % q)
+            pws[q] = bank("pw%d" % q)
             for i in range(4):
                 a, u = i // 2, i % 2
                 words = w_sb[:, q, a, :].bitcast(F32)
@@ -201,7 +210,7 @@ def tile_tubeletembedding_kernel(tc, video, W, b, pos_embed, out):
             nc.vector.quantize_mx(out=wc[:, c0:c0 + n].bitcast(FP8X4), scales=ws[:, c0:c0 + n], in_=gw[:, 4 * c0:4 * (c0 + n)])
 
         def mx(t, h):
-            acc = bank("acc", "acc%d_%d" % (t, h))
+            acc = bank("acc%d_%d" % (t, h))
             nc.tensor.matmul_mx(
                 out=acc[:],
                 lhsT=tokc[:, t * P:(t + 1) * P].bitcast(FP8X4), lhsT_scale=toks[:, t * P:(t + 1) * P],
@@ -232,104 +241,106 @@ def tile_tubeletembedding_kernel(tc, video, W, b, pos_embed, out):
             nc.sync.dma_start(out=dram(t, cols), in_=o_sb[t][:, cols])
 
         warm(4)
+        bias_columns()
+        bias_spread(0)
         regroup(0, 0)
         regroup(0, 1)
+        posb_v(0, 0)
         load_b()
+        load_w(2, 4)
         load_pos(1)
         w_t(0)
         w_c(0, "S")
         a23 = tok_a(2)
         copy_out("V", g_l, a23[:, 1])
-        copy_out("V", g_0[:, :, 2:4, :], a23[:, 0])
+        quant_w(0, 256)
         w_t(1)
         w_c(1, "S")
         a01 = tok_a(0)
         quant_tok(0, 128)
+        copy_out("V", g_0[:, :, 2:4, :], a23[:, 0])
         copy_out("S", g_0[:, :, 0:2, :], a01[:, 0])
         copy_out("S", g_0[:, :, 6:8, :], a01[:, 1])
         a45 = tok_a(4)
-        quant_w(0, 256)
-        copy_out("V", g_0[:, :, 4:6, :], a45[:, 0])
         quant_w(256, 256)
+        copy_out("V", g_0[:, :, 4:6, :], a45[:, 0])
         pn_mm(0)
         pn_copy(0)
-        bbc_mm(0)
-        w_t(2)
-        w_c(2, "S")
+        bias_spread(1)
         mx(0, 0)
-        w_t(3)
         quant_tok(128, 512)
-        add_sg(0, 0)
-        posb_v(0, 0)
-        copy_out("V", g_1[:, :, 0:2, :], a45[:, 1])
-        w_c(3, "S")
+        w_t(2)
+        regroup(1, 1, "S")
+        add_v(0, 0)
+        store(0, 0)
+        regroup(1, 0)
+        w_c(2, "S")
         mx(1, 0)
+        w_t(3)
+        w_c(3, "S")
         mx(2, 0)
-        mx(3, 0)
-        bbc_mm(1)
         add_v(1, 0)
         store(1, 0)
-        add_sg(3, 0)
-        add_v(2, 0)
-        store(2, 0)
-        store(0, 0)
-        quant_w(512, 512)
-        mx(4, 0)
-        regroup(1, 0, "S")
-        posb_v(0, 1)
-        mx(1, 1)
-        mx(2, 1)
-        mx(0, 1)
-        add_v(4, 0)
-        store(4, 0)
-        regroup(1, 1, "S2")
-        pn_mm(1)
-        pn_copy(1)
-        add_sg(0, 1)
-        store(3, 0)
-        add_v(1, 1)
-        store(1, 1)
-        bbc_mm(0)
-        bbc_mm(1)
+        mx(3, 0)
+        add_sg(2, 0)
+        copy_out("V", g_1[:, :, 0:2, :], a45[:, 1])
         b01 = tok_b(0)
         b23 = tok_b(2)
+        add_v(3, 0)
+        store(3, 0)
+        mx(4, 0)
         b45 = tok_b(4)
-        mx(3, 1)
-        mx(4, 1)
-        add_v(2, 1)
-        store(2, 1)
+        quant_w(512, 512)
         copy_out("S", g_1[:, :, 2:4, :], b01)
         copy_out("S", g_1[:, :, 4:6, :], b23)
         copy_out("S", g_1[:, :, 6:8, :], b45)
-        posb_v(1, 0)
-        store(0, 1)
-        add_sg(4, 1)
+        pn_mm(1)
+        mx(0, 1)
+        pp_mm(1, 0)
+        add_v(4, 0)
+        store(4, 0)
+        pn_copy(1)
+        posb_v(0, 1)
+        store(2, 0)
+        add_sg(0, 1)
+        mx(1, 1)
+        mx(2, 1)
+        mx(3, 1)
         quant_tok(640, 512)
-        posb_v(1, 1)
+        pp_copy(1, 0)
+        add_v(1, 1)
+        store(1, 1)
+        add_sg(2, 1)
         mx(5, 0)
         mx(6, 0)
-        mx(7, 0)
         add_v(3, 1)
         store(3, 1)
-        add_sg(6, 0)
+        store(0, 1)
+        mx(4, 1)
         add_v(5, 0)
         store(5, 0)
-        store(4, 1)
+        pp_mm(1, 1)
+        add_sg(4, 1)
+        mx(7, 0)
+        pp_copy(1, 1)
+        add_v(6, 0)
+        store(6, 0)
         mx(8, 0)
-        mx(5, 1)
+        mx(6, 1)
+        store(2, 1)
         add_v(7, 0)
         store(7, 0)
-        mx(6, 1)
-        add_sg(8, 0)
-        store(6, 0)
+        add_sg(6, 1)
+        mx(5, 1)
         mx(7, 1)
-        mx(8, 1)
+        add_v(8, 0)
+        store(8, 0)
+        store(4, 1)
         add_v(5, 1)
         store(5, 1)
-        add_sg(6, 1)
-        store(8, 0)
+        mx(8, 1)
         add_v(7, 1)
         store(7, 1)
-        add_v(8, 1)
         store(6, 1)
+        add_v(8, 1)
         store(8, 1)

@@ -96,7 +96,6 @@ def tile_tubeletembedding_kernel(tc, video, W, b, pos_embed, out):
         ws = keep.tile([P, 1024], U8, align_bytes=64)
         posb = [keep.tile([P, 1024], F32, name="posb%d" % g) for g in range(3)]
         o_sb = [keep.tile([P, 1024], F32, name="o%d" % t) for t in range(9)]
-        bbcs = keep.tile([P, 1024], F32)
         accs = {}
         order = []
 
@@ -114,19 +113,20 @@ def tile_tubeletembedding_kernel(tc, video, W, b, pos_embed, out):
             else:
                 nc.scalar.copy(out=dst, in_=src)
 
-        def warm(n):
-            pw = bank("warm")
+        def keep_clock(pt, n):
             for i in range(n):
-                nc.tensor.matmul(out=pw[:, i * P:(i + 1) * P], lhsT=ident[:], rhs=ident[:], start=True, stop=True)
+                nc.tensor.matmul(out=pt[:, 0:64], lhsT=ident[:], rhs=ident[:, 0:64], start=True, stop=True)
 
         bt = keep.tile([P, 8], BF16)
         bbt = psum.tile([P, 1024], BF16, tag="bbt")
 
-        def bias_columns():
+        def bias_columns(n, m):
             pt = bank("pbt")
+            keep_clock(pt, n)
             ph = pt[:].bitcast(BF16)
             nc.tensor.transpose(ph[:, 0:P], b8[:], ident_h[:])
             nc.scalar.copy(out=bt[:], in_=ph[:, 0:8])
+            keep_clock(pt[:, 256:512], m)
 
         def bias_spread(h):
             for m in range(4 * h, 4 * h + 4):
@@ -134,15 +134,13 @@ def tile_tubeletembedding_kernel(tc, video, W, b, pos_embed, out):
 
         pns = {}
 
-        def pn_mm(h):
+        def pn_mm(h, n=0):
             pns[h] = bank("pn%d" % h)
+            keep_clock(pns[h], n)
             nc.tensor.matmul(out=pns[h][:], lhsT=sel_n[:], rhs=z[:, half(h)], start=True, stop=True)
 
         def pn_copy(h):
             nc.scalar.copy(out=posb[2][:, half(h)], in_=pns[h][:])
-
-        def posb_g(g, h):
-            nc.gpsimd.tensor_tensor(out=posb[g][:, half(h)], in0=pos_sb[g][:, half(h)], in1=bbcs[:, half(h)], op=ADD)
 
         def posb_v(g, h):
             nc.vector.tensor_tensor(out=posb[g][:, half(h)], in0=bbt[:, half(h)], in1=pos_sb[g][:, half(h)], op=ADD)
@@ -167,8 +165,9 @@ def tile_tubeletembedding_kernel(tc, video, W, b, pos_embed, out):
                 for u in range(2):
                     copy_out(eng, dst[:, t, :, u], src[:, :, u])
 
-        def tok_a(j0):
+        def tok_a(j0, n=0):
             pt = bank("pa%d" % j0)
+            keep_clock(pt, n)
             vw = v2[0][:].bitcast(F32)
             for i in range(4):
                 r = 2 * j0 + i
@@ -189,8 +188,9 @@ def tile_tubeletembedding_kernel(tc, video, W, b, pos_embed, out):
 
         pws = {}
 
-        def w_t(q):
+        def w_t(q, n=0):
             pws[q] = bank("pw%d" % q)
+            keep_clock(pws[q], n)
             for i in range(4):
                 a, u = i // 2, i % 2
                 words = w_sb[:, q, a, :].bitcast(F32)
@@ -240,8 +240,7 @@ def tile_tubeletembedding_kernel(tc, video, W, b, pos_embed, out):
             cols = slice(0, 1024) if h is None else half(h)
             nc.sync.dma_start(out=dram(t, cols), in_=o_sb[t][:, cols])
 
-        warm(4)
-        bias_columns()
+        bias_columns(8, 4)
         bias_spread(0)
         regroup(0, 0)
         regroup(0, 1)
@@ -249,19 +248,19 @@ def tile_tubeletembedding_kernel(tc, video, W, b, pos_embed, out):
         load_b()
         load_w(2, 4)
         load_pos(1)
-        w_t(0)
+        w_t(0, 0)
         w_c(0, "S")
-        a23 = tok_a(2)
+        a23 = tok_a(2, 1)
         copy_out("V", g_l, a23[:, 1])
         quant_w(0, 256)
-        w_t(1)
+        w_t(1, 1)
         w_c(1, "S")
-        a01 = tok_a(0)
+        a01 = tok_a(0, 1)
         quant_tok(0, 128)
         copy_out("V", g_0[:, :, 2:4, :], a23[:, 0])
         copy_out("S", g_0[:, :, 0:2, :], a01[:, 0])
         copy_out("S", g_0[:, :, 6:8, :], a01[:, 1])
-        a45 = tok_a(4)
+        a45 = tok_a(4, 1)
         quant_w(256, 256)
         copy_out("V", g_0[:, :, 4:6, :], a45[:, 0])
         pn_mm(0)
@@ -269,7 +268,7 @@ def tile_tubeletembedding_kernel(tc, video, W, b, pos_embed, out):
         bias_spread(1)
         mx(0, 0)
         quant_tok(128, 512)
-        w_t(2)
+        w_t(2, 0)
         regroup(1, 1, "S")
         add_v(0, 0)
         store(0, 0)
@@ -282,47 +281,46 @@ def tile_tubeletembedding_kernel(tc, video, W, b, pos_embed, out):
         add_v(1, 0)
         store(1, 0)
         mx(3, 0)
-        add_sg(2, 0)
         copy_out("V", g_1[:, :, 0:2, :], a45[:, 1])
+        add_sg(2, 0)
         b01 = tok_b(0)
         b23 = tok_b(2)
-        add_v(3, 0)
-        store(3, 0)
+        quant_w(512, 512)
         mx(4, 0)
         b45 = tok_b(4)
-        quant_w(512, 512)
+        add_v(3, 0)
+        store(3, 0)
         copy_out("S", g_1[:, :, 2:4, :], b01)
         copy_out("S", g_1[:, :, 4:6, :], b23)
         copy_out("S", g_1[:, :, 6:8, :], b45)
         pn_mm(1)
         mx(0, 1)
-        pp_mm(1, 0)
         add_v(4, 0)
         store(4, 0)
-        pn_copy(1)
-        posb_v(0, 1)
         store(2, 0)
+        pn_copy(1)
+        quant_tok(640, 512)
         add_sg(0, 1)
+        posb_v(0, 1)
         mx(1, 1)
         mx(2, 1)
         mx(3, 1)
-        quant_tok(640, 512)
-        pp_copy(1, 0)
         add_v(1, 1)
         store(1, 1)
         add_sg(2, 1)
+        posb_v(1, 0)
         mx(5, 0)
         mx(6, 0)
         add_v(3, 1)
         store(3, 1)
         store(0, 1)
+        pp_mm(1, 1)
         mx(4, 1)
         add_v(5, 0)
         store(5, 0)
-        pp_mm(1, 1)
         add_sg(4, 1)
-        mx(7, 0)
         pp_copy(1, 1)
+        mx(7, 0)
         add_v(6, 0)
         store(6, 0)
         mx(8, 0)

@@ -115,7 +115,7 @@ def tile_tubeletembedding_kernel(tc, video, W, b, pos_embed, out):
 
         def keep_clock(pt, n):
             for i in range(n):
-                nc.tensor.matmul(out=pt[:, 0:64], lhsT=ident[:], rhs=ident[:, 0:64], start=True, stop=True)
+                nc.tensor.matmul(out=pt[:, 0:P], lhsT=ident[:], rhs=ident[:], start=True, stop=True)
 
         bt = keep.tile([P, 8], BF16)
         bbt = psum.tile([P, 1024], BF16, tag="bbt")
@@ -240,22 +240,22 @@ def tile_tubeletembedding_kernel(tc, video, W, b, pos_embed, out):
             cols = slice(0, 1024) if h is None else half(h)
             nc.sync.dma_start(out=dram(t, cols), in_=o_sb[t][:, cols])
 
-        bias_columns(8, 4)
+        bias_columns(4, 2)
         bias_spread(0)
         regroup(0, 0)
         regroup(0, 1)
         posb_v(0, 0)
-        load_b()
         load_w(2, 4)
+        load_b()
         load_pos(1)
         w_t(0, 0)
         w_c(0, "S")
-        a23 = tok_a(2, 1)
+        a23 = tok_a(2, 0)
         copy_out("V", g_l, a23[:, 1])
         quant_w(0, 256)
         w_t(1, 1)
         w_c(1, "S")
-        a01 = tok_a(0, 1)
+        a01 = tok_a(0, 0)
         quant_tok(0, 128)
         copy_out("V", g_0[:, :, 2:4, :], a23[:, 0])
         copy_out("S", g_0[:, :, 0:2, :], a01[:, 0])
@@ -265,78 +265,78 @@ def tile_tubeletembedding_kernel(tc, video, W, b, pos_embed, out):
         copy_out("V", g_0[:, :, 4:6, :], a45[:, 0])
         pn_mm(0)
         pn_copy(0)
-        bias_spread(1)
+        copy_out("S", g_1[:, :, 0:2, :], a45[:, 1])
+        w_t(2, 0)
         mx(0, 0)
         quant_tok(128, 512)
-        w_t(2, 0)
-        regroup(1, 1, "S")
+        w_c(2, "S")
+        w_t(3, 0)
         add_v(0, 0)
         store(0, 0)
         regroup(1, 0)
-        w_c(2, "S")
         mx(1, 0)
-        w_t(3)
-        w_c(3, "S")
         mx(2, 0)
+        mx(3, 0)
+        w_c(3, "S")
         add_v(1, 0)
         store(1, 0)
-        mx(3, 0)
-        copy_out("V", g_1[:, :, 0:2, :], a45[:, 1])
-        add_sg(2, 0)
-        b01 = tok_b(0)
-        b23 = tok_b(2)
         quant_w(512, 512)
         mx(4, 0)
-        b45 = tok_b(4)
+        pn_mm(1)
+        add_sg(2, 0)
+        bias_spread(1)
         add_v(3, 0)
         store(3, 0)
-        copy_out("S", g_1[:, :, 2:4, :], b01)
-        copy_out("S", g_1[:, :, 4:6, :], b23)
-        copy_out("S", g_1[:, :, 6:8, :], b45)
-        pn_mm(1)
+        regroup(1, 1, "S")
+        pn_copy(1)
         mx(0, 1)
         add_v(4, 0)
         store(4, 0)
-        store(2, 0)
-        pn_copy(1)
-        quant_tok(640, 512)
-        add_sg(0, 1)
         posb_v(0, 1)
         mx(1, 1)
+        store(2, 0)
+        add_v(0, 1)
+        store(0, 1)
+        b01 = tok_b(0)
+        b23 = tok_b(2)
+        b45 = tok_b(4)
+        copy_out("S", g_1[:, :, 2:4, :], b01)
+        copy_out("S", g_1[:, :, 4:6, :], b23)
+        copy_out("S", g_1[:, :, 6:8, :], b45)
         mx(2, 1)
         mx(3, 1)
         add_v(1, 1)
         store(1, 1)
         add_sg(2, 1)
-        posb_v(1, 0)
-        mx(5, 0)
-        mx(6, 0)
+        quant_tok(640, 512)
+        mx(4, 1)
         add_v(3, 1)
         store(3, 1)
-        store(0, 1)
+        add_sg(4, 1)
+        posb_v(1, 0)
         pp_mm(1, 1)
-        mx(4, 1)
+        mx(5, 0)
+        mx(6, 0)
+        pp_copy(1, 1)
+        store(2, 1)
         add_v(5, 0)
         store(5, 0)
-        add_sg(4, 1)
-        pp_copy(1, 1)
         mx(7, 0)
-        add_v(6, 0)
-        store(6, 0)
+        add_sg(6, 0)
+        store(4, 1)
         mx(8, 0)
-        mx(6, 1)
-        store(2, 1)
+        mx(5, 1)
         add_v(7, 0)
         store(7, 0)
-        add_sg(6, 1)
-        mx(5, 1)
-        mx(7, 1)
+        mx(6, 1)
         add_v(8, 0)
         store(8, 0)
-        store(4, 1)
+        store(6, 0)
+        add_sg(6, 1)
+        mx(7, 1)
+        mx(8, 1)
         add_v(5, 1)
         store(5, 1)
-        mx(8, 1)
         add_v(7, 1)
         store(7, 1)
         store(6, 1)

@@ -20,16 +20,17 @@ def tile_tubeletembedding_kernel(tc, video, W, b, pos_embed, out):
         psum = ctx.enter_context(tc.psum_pool(name="psum", bufs=1))
         ctx.enter_context(tc.manual_schedule())
 
-        vid = video.rearrange("b (d t) o (h c y) x -> t c (b d) h (o y x)", t=2, h=2, c=3, y=16)
+        vid = video.rearrange("b (d t) o (i y) x -> t (b d) i (o y x)", t=2, i=6)
         wv = W.rearrange("(q p a) k -> p q a k", q=4, a=2)
-        pv = pos_embed.rearrange("o (s r) e -> (o s) r e", r=18)
-        ov = out.rearrange("b (s r) e -> b s r e", r=18)
-        on = out.rearrange("b (s r) e -> (b s) r e", r=18)
+        pv = pos_embed.rearrange("o (d r) e -> (o d) r e", r=36)
+        pr = pos_embed.rearrange("o (d r) e -> r (o d) e", r=36)
+        ov = out.rearrange("b (d r) e -> b r d e", r=36)
+        on = out.rearrange("b (d r) e -> (b d) r e", r=36)
 
         ident = keep.tile([P, P], F32)
         make_identity(nc, ident[:])
-        b8 = keep.tile([P, P], BF16)
-        nc.vector.memset(b8[:].bitcast(U32), 0)
+        zb = keep.tile([P, 1024], BF16)
+        nc.vector.memset(zb[:].bitcast(U32), 0)
         z = keep.tile([P, 1024], BF16)
         nc.vector.memset(z[:].bitcast(U32), 0)
 
@@ -38,29 +39,28 @@ def tile_tubeletembedding_kernel(tc, video, W, b, pos_embed, out):
         pos_sb = [keep.tile([P, 1024], BF16, name="pos%d" % g) for g in range(2)]
 
         def load_a(t):
-            for c in range(2):
-                nc.sync.dma_start(out=v_sb[t][c:P:2, :], in_=vid[t, c])
+            nc.sync.dma_start(out=v_sb[t][:], in_=vid[t, :, 0:4, :])
 
         def load_b():
             for t in range(2):
-                nc.sync.dma_start(out=v_sb[t][0:P:2, :], in_=vid[t, 2])
+                nc.sync.dma_start(out=v_sb[t][0:P:2, :], in_=vid[t, :, 4:6, :])
 
         def load_w(q0, q1):
             nc.sync.dma_start(out=w_sb[:, q0:q1], in_=wv[:, q0:q1])
 
+        def load_zb():
+            nc.sync.dma_start(out=zb[32:33, :], in_=b.unsqueeze(0))
+
         def load_z():
             nc.sync.dma_start(out=z[32:33, :], in_=b.unsqueeze(0))
-            nc.sync.dma_start(out=z[0:32, :], in_=pv[:, 8:10, :])
-
-        def load_b8():
-            nc.sync.dma_start(out=b8[0:8, :], in_=b.rearrange("(m e) -> m e", m=8))
+            nc.sync.dma_start(out=z[0:32, :], in_=pv[:, 0:4, :])
 
         def load_pos(g, h=None):
             cols = slice(0, 1024) if h is None else slice(h * 512, (h + 1) * 512)
-            nc.sync.dma_start(out=pos_sb[g][:, cols], in_=pv[:, 10 * g:10 * g + 8, cols])
+            nc.sync.dma_start(out=pos_sb[g][:, cols], in_=pr[4 + 16 * g:20 + 16 * g, :, cols])
 
         load_a(0)
-        load_b8()
+        load_zb()
         load_a(1)
         load_w(0, 1)
         load_pos(0, 0)
@@ -68,10 +68,10 @@ def tile_tubeletembedding_kernel(tc, video, W, b, pos_embed, out):
         load_z()
         load_pos(0, 1)
 
-        perm = keep.tile([P, P], F32)
+        perm_a = keep.tile([P, P], F32)
         nc.vector.tensor_copy(
-            out=perm[:].rearrange("p (c x) -> p c x", c=2),
-            in_=ident[:].rearrange("p (x c) -> p c x", c=2),
+            out=perm_a[:].rearrange("p (i x) -> p i x", i=4),
+            in_=ident[:].rearrange("p (x i) -> p i x", i=4),
         )
         sel_b = keep.tile([P, P], BF16)
         nc.vector.tensor_copy(out=sel_b[:], in_=ident[:, 32:33].to_broadcast([P, P]))
@@ -82,8 +82,11 @@ def tile_tubeletembedding_kernel(tc, video, W, b, pos_embed, out):
             in1=ident[:, 32:33].unsqueeze(1).to_broadcast([P, 4, 32]),
             op=ADD,
         )
-        ident_h = keep.tile([P, P], BF16)
-        nc.vector.tensor_copy(out=ident_h[:], in_=ident[:])
+        perm_b = keep.tile([P, P], F32)
+        nc.vector.tensor_copy(
+            out=perm_b[:].rearrange("p (z i x) -> p z i x", z=2, i=2),
+            in_=ident[:].rearrange("p (x i z) -> p z i x", i=2, z=2),
+        )
 
         v2 = [keep.tile([P, 3072], BF16, name="v2_%d" % s) for s in range(2)]
         grp = keep.tile([P, 4608], BF16, align_bytes=64)
@@ -103,7 +106,6 @@ def tile_tubeletembedding_kernel(tc, video, W, b, pos_embed, out):
             order.append(name)
             return psum.tile([P, 512], F32, tag="bank%d" % (len(order) % 7), name=name)
 
-
         def half(h):
             return slice(h * 512, (h + 1) * 512)
 
@@ -117,53 +119,29 @@ def tile_tubeletembedding_kernel(tc, video, W, b, pos_embed, out):
             for i in range(n):
                 nc.tensor.matmul(out=pt[:, 0:P], lhsT=ident[:], rhs=ident[:], start=True, stop=True)
 
-        bt = keep.tile([P, 8], BF16)
         bbt = psum.tile([P, 1024], BF16, tag="bbt")
 
-        def bias_columns(n, m):
-            pt = bank("pbt")
-            keep_clock(pt, n)
-            ph = pt[:].bitcast(BF16)
-            nc.tensor.transpose(ph[:, 0:P], b8[:], ident_h[:])
-            nc.scalar.copy(out=bt[:], in_=ph[:, 0:8])
-            keep_clock(pt[:, 256:512], m)
-
         def bias_spread(h):
-            for m in range(4 * h, 4 * h + 4):
-                nc.tensor.transpose(bbt[:, m * P:(m + 1) * P], bt[:, m:m + 1].to_broadcast([P, P]), ident_h[:])
+            nc.tensor.matmul(out=bbt[:, half(h)], lhsT=sel_b[:], rhs=zb[:, half(h)], start=True, stop=True)
 
         pns = {}
 
-        def pn_mm(h, n=0):
+        def pn_mm(h):
             pns[h] = bank("pn%d" % h)
-            keep_clock(pns[h], n)
             nc.tensor.matmul(out=pns[h][:], lhsT=sel_n[:], rhs=z[:, half(h)], start=True, stop=True)
 
         def pn_copy(h):
             nc.scalar.copy(out=posb[2][:, half(h)], in_=pns[h][:])
 
-        def posb_v(g, h):
-            nc.vector.tensor_tensor(out=posb[g][:, half(h)], in0=bbt[:, half(h)], in1=pos_sb[g][:, half(h)], op=ADD)
+        def posb_v(g, c0, c1):
+            cols = slice(c0, c1)
+            nc.vector.tensor_tensor(out=posb[g][:, cols], in0=bbt[:, cols], in1=pos_sb[g][:, cols], op=ADD)
 
-        pps = {}
-
-        def pp_mm(g, h):
-            pps[(g, h)] = bank("pp%d_%d" % (g, h))
-            nc.tensor.matmul(out=pps[(g, h)][:], lhsT=ident_h[:], rhs=pos_sb[g][:, half(h)], start=True, stop=False)
-            nc.tensor.matmul(out=pps[(g, h)][:], lhsT=sel_b[:], rhs=z[:, half(h)], start=False, stop=True)
-
-        def pp_copy(g, h):
-            nc.scalar.copy(out=posb[g][:, half(h)], in_=pps[(g, h)][:])
-
-        def regroup(s, t, eng="V"):
+        def regroup(s, t, eng="V", j0=0, j1=6):
             dst = v2[s][:].bitcast(F32).rearrange("p (j u t y x) -> p t j u y x", j=6, u=2, t=2, y=16)
             src = v_sb[t][:].bitcast(F32).rearrange("p (y j x u) -> p j u y x", y=16, j=6, u=2)
-            if eng == "S2":
-                copy_out("V", dst[:, t, :, 0], src[:, :, 0])
-                copy_out("S", dst[:, t, :, 1], src[:, :, 1])
-            else:
-                for u in range(2):
-                    copy_out(eng, dst[:, t, :, u], src[:, :, u])
+            for u in range(2):
+                copy_out(eng, dst[:, t, j0:j1, u], src[:, j0:j1, u])
 
         def tok_a(j0, n=0):
             pt = bank("pa%d" % j0)
@@ -171,20 +149,27 @@ def tile_tubeletembedding_kernel(tc, video, W, b, pos_embed, out):
             vw = v2[0][:].bitcast(F32)
             for i in range(4):
                 r = 2 * j0 + i
-                nc.tensor.transpose(pt[:, i * P:(i + 1) * P], vw[:, r * P:(r + 1) * P], perm[:])
-            return pt[:].rearrange("p (j u c x) -> p c x j u", j=2, u=2, c=2)
+                nc.tensor.transpose(pt[:, i * P:(i + 1) * P], vw[:, r * P:(r + 1) * P], perm_a[:])
+            return pt[:].rearrange("p (j u i b d) -> p i b j d u", j=2, u=2, i=4, b=4)
 
         def tok_b(j0):
             pt = bank("pb%d" % j0)
             vw = v2[1][:].bitcast(F32)
             for i in range(4):
                 r = 2 * j0 + i
-                nc.tensor.transpose(pt[:, i * 64:i * 64 + P], vw[:, r * P:(r + 1) * P], perm[:])
-            return pt[:, 0:256].rearrange("p (j u x) -> p x j u", j=2, u=2)
+                nc.tensor.transpose(pt[:, i * 64:i * 64 + P], vw[:, r * P:(r + 1) * P], perm_b[:])
+            return pt[:, 0:256].rearrange("p (j u i b d) -> p i b j d u", j=2, u=2, i=2, b=4)
 
-        g_l = grpw[:, 0:256].rearrange("p (x r u) -> p x r u", r=2, u=2)
-        g_0 = grpw[:, 256:1280].rearrange("p (x r u) -> p x r u", r=8, u=2)
-        g_1 = grpw[:, 1280:2304].rearrange("p (x r u) -> p x r u", r=8, u=2)
+        g_l = grpw[:, 0:256].rearrange("p (b d r u) -> p b r d u", b=4, r=4, u=2)
+        g_t = [grpw[:, 256 + g * 1024:1280 + g * 1024].rearrange("p (b r d u) -> p b r d u", b=4, r=16, u=2) for g in range(2)]
+
+        def put(eng, src, i, r):
+            if r < 4:
+                dst = g_l[:, :, r:r + 2]
+            else:
+                g, r0 = (r - 4) // 16, (r - 4) % 16
+                dst = g_t[g][:, :, r0:r0 + 2]
+            copy_out(eng, dst, src[:, i])
 
         pws = {}
 
@@ -232,45 +217,52 @@ def tile_tubeletembedding_kernel(tc, video, W, b, pos_embed, out):
 
         def dram(t, cols):
             if t == 0:
-                return on[:, 8:10, cols]
+                return on[:, 0:4, cols]
             g, bi = (t - 1) // 4, (t - 1) % 4
-            return ov[bi, :, 10 * g:10 * g + 8, cols]
+            return ov[bi, 4 + 16 * g:20 + 16 * g, :, cols]
 
         def store(t, h=None):
             cols = slice(0, 1024) if h is None else half(h)
             nc.sync.dma_start(out=dram(t, cols), in_=o_sb[t][:, cols])
 
-        bias_columns(4, 2)
+        keep_clock(bank("clock"), 4)
         bias_spread(0)
+        bias_spread(1)
         regroup(0, 0)
         regroup(0, 1)
-        posb_v(0, 0)
+        posb_v(0, 0, 512)
         load_w(2, 4)
         load_b()
         load_pos(1)
         w_t(0, 0)
-        w_c(0, "S")
-        a23 = tok_a(2, 0)
-        copy_out("V", g_l, a23[:, 1])
-        quant_w(0, 256)
-        w_t(1, 1)
-        w_c(1, "S")
         a01 = tok_a(0, 0)
+        w_c(0, "S")
+        put("V", a01, 0, 0)
+        put("V", a01, 1, 6)
+        put("V", a01, 2, 12)
+        put("V", a01, 3, 18)
+        w_t(1, 1)
+        quant_w(0, 256)
+        a23 = tok_a(2, 0)
+        w_c(1, "S")
+        put("V", a23, 0, 2)
         quant_tok(0, 128)
-        copy_out("V", g_0[:, :, 2:4, :], a23[:, 0])
-        copy_out("S", g_0[:, :, 0:2, :], a01[:, 0])
-        copy_out("S", g_0[:, :, 6:8, :], a01[:, 1])
+        put("V", a23, 1, 8)
+        put("V", a23, 2, 14)
         a45 = tok_a(4, 1)
         quant_w(256, 256)
-        copy_out("V", g_0[:, :, 4:6, :], a45[:, 0])
+        put("S", a45, 0, 4)
+        put("S", a45, 1, 10)
+        put("S", a45, 2, 16)
+        put("V", a23, 3, 20)
         pn_mm(0)
         pn_copy(0)
-        copy_out("S", g_1[:, :, 0:2, :], a45[:, 1])
-        w_t(2, 0)
+        put("S", a45, 3, 22)
+        w_t(2)
         mx(0, 0)
         quant_tok(128, 512)
         w_c(2, "S")
-        w_t(3, 0)
+        w_t(3)
         add_v(0, 0)
         store(0, 0)
         regroup(1, 0)
@@ -284,7 +276,6 @@ def tile_tubeletembedding_kernel(tc, video, W, b, pos_embed, out):
         mx(4, 0)
         pn_mm(1)
         add_sg(2, 0)
-        bias_spread(1)
         add_v(3, 0)
         store(3, 0)
         regroup(1, 1, "S")
@@ -292,7 +283,7 @@ def tile_tubeletembedding_kernel(tc, video, W, b, pos_embed, out):
         mx(0, 1)
         add_v(4, 0)
         store(4, 0)
-        posb_v(0, 1)
+        posb_v(0, 512, 1024)
         mx(1, 1)
         store(2, 0)
         add_v(0, 1)
@@ -300,24 +291,25 @@ def tile_tubeletembedding_kernel(tc, video, W, b, pos_embed, out):
         b01 = tok_b(0)
         b23 = tok_b(2)
         b45 = tok_b(4)
-        copy_out("S", g_1[:, :, 2:4, :], b01)
-        copy_out("S", g_1[:, :, 4:6, :], b23)
-        copy_out("S", g_1[:, :, 6:8, :], b45)
+        put("S", b01, 0, 24)
+        put("S", b01, 1, 30)
+        put("S", b23, 0, 26)
+        put("S", b23, 1, 32)
+        put("S", b45, 0, 28)
+        put("S", b45, 1, 34)
         mx(2, 1)
         mx(3, 1)
         add_v(1, 1)
         store(1, 1)
-        add_sg(2, 1)
         quant_tok(640, 512)
+        add_sg(2, 1)
         mx(4, 1)
         add_v(3, 1)
         store(3, 1)
         add_sg(4, 1)
-        posb_v(1, 0)
-        pp_mm(1, 1)
+        posb_v(1, 0, 512)
         mx(5, 0)
         mx(6, 0)
-        pp_copy(1, 1)
         store(2, 1)
         add_v(5, 0)
         store(5, 0)
@@ -332,6 +324,7 @@ def tile_tubeletembedding_kernel(tc, video, W, b, pos_embed, out):
         add_v(8, 0)
         store(8, 0)
         store(6, 0)
+        posb_v(1, 512, 1024)
         add_sg(6, 1)
         mx(7, 1)
         mx(8, 1)

from contextlib import ExitStack

import concourse.mybir as mybir
from concourse.masks import make_identity

F32 = mybir.dt.float32
BF16 = mybir.dt.bfloat16
U32 = mybir.dt.uint32
U8 = mybir.dt.uint8
FP8X4 = mybir.dt.float8_e4m3fn_x4
ADD = mybir.AluOpType.add
P = 128
FLOPS = 2 * 1152 * 512 * 1024


def tile_tubeletembedding_kernel(tc, video, W, b, pos_embed, out):
    nc = tc.nc
    with ExitStack() as ctx:
        keep = ctx.enter_context(tc.tile_pool(name="keep", bufs=1))
        psum = ctx.enter_context(tc.psum_pool(name="psum", bufs=1))
        ctx.enter_context(tc.manual_schedule())

        vid = video.rearrange("b (d t) o (i y) x -> t (b d) i (o y x)", t=2, i=6)
        wv = W.rearrange("(q p a) k -> p q a k", q=4, a=2)
        pv = pos_embed.rearrange("o (d r) e -> (o d) r e", r=36)
        pr = pos_embed.rearrange("o (d r) e -> r (o d) e", r=36)
        ov = out.rearrange("b (d r) e -> b r d e", r=36)
        on = out.rearrange("b (d r) e -> (b d) r e", r=36)

        ident = keep.tile([P, P], F32)
        make_identity(nc, ident[:])
        zb = keep.tile([P, 1024], BF16)
        nc.vector.memset(zb[:].bitcast(U32), 0)
        z = keep.tile([P, 1024], BF16)
        nc.vector.memset(z[:].bitcast(U32), 0)

        v_sb = [keep.tile([P, 1536], BF16, name="v%d" % t) for t in range(2)]
        w_sb = keep.tile([P, 4, 2, 512], BF16)
        pos_sb = [keep.tile([P, 1024], BF16, name="pos%d" % g) for g in range(2)]

        def load_a(t):
            nc.sync.dma_start(out=v_sb[t][:], in_=vid[t, :, 0:4, :])

        def load_b():
            for t in range(2):
                nc.sync.dma_start(out=v_sb[t][0:P:2, :], in_=vid[t, :, 4:6, :])

        def load_w(q0, q1):
            nc.sync.dma_start(out=w_sb[:, q0:q1], in_=wv[:, q0:q1])

        def load_zb():
            nc.sync.dma_start(out=zb[32:33, :], in_=b.unsqueeze(0))

        def load_z():
            nc.sync.dma_start(out=z[32:33, :], in_=b.unsqueeze(0))
            nc.sync.dma_start(out=z[0:32, :], in_=pv[:, 0:4, :])

        def load_pos(g, h=None):
            cols = slice(0, 1024) if h is None else slice(h * 512, (h + 1) * 512)
            nc.sync.dma_start(out=pos_sb[g][:, cols], in_=pr[4 + 16 * g:20 + 16 * g, :, cols])

        load_a(0)
        load_zb()
        load_a(1)
        load_w(0, 1)
        load_pos(0, 0)
        load_w(1, 2)
        load_z()
        load_pos(0, 1)

        perm_a = keep.tile([P, P], F32)
        nc.vector.tensor_copy(
            out=perm_a[:].rearrange("p (i x) -> p i x", i=4),
            in_=ident[:].rearrange("p (x i) -> p i x", i=4),
        )
        sel_b = keep.tile([P, P], BF16)
        nc.vector.tensor_copy(out=sel_b[:], in_=ident[:, 32:33].to_broadcast([P, P]))
        sel_n = keep.tile([P, P], BF16)
        nc.vector.tensor_tensor(
            out=sel_n[:].rearrange("p (c q) -> p c q", c=4),
            in0=ident[:, 0:32].unsqueeze(1).to_broadcast([P, 4, 32]),
            in1=ident[:, 32:33].unsqueeze(1).to_broadcast([P, 4, 32]),
            op=ADD,
        )
        perm_b = keep.tile([P, P], F32)
        nc.vector.tensor_copy(
            out=perm_b[:].rearrange("p (z i x) -> p z i x", z=2, i=2),
            in_=ident[:].rearrange("p (x i z) -> p z i x", i=2, z=2),
        )

        v2 = [keep.tile([P, 3072], BF16, name="v2_%d" % s) for s in range(2)]
        grp = keep.tile([P, 4608], BF16, align_bytes=64)
        grpw = grp[:].bitcast(F32)
        tokc = keep.tile([P, 1152], U32, align_bytes=64)
        toks = keep.tile([P, 1152], U8, align_bytes=64)
        gw = keep.tile([P, 4096], BF16, align_bytes=64)
        gww = gw[:].bitcast(F32)
        wc = keep.tile([P, 1024], U32, align_bytes=64)
        ws = keep.tile([P, 1024], U8, align_bytes=64)
        posb = [keep.tile([P, 1024], F32, name="posb%d" % g) for g in range(3)]
        o_sb = [keep.tile([P, 1024], F32, name="o%d" % t) for t in range(9)]
        accs = {}
        order = []

        def bank(name):
            order.append(name)
            return psum.tile([P, 512], F32, tag="bank%d" % (len(order) % 7), name=name)

        def half(h):
            return slice(h * 512, (h + 1) * 512)

        def copy_out(eng, dst, src):
            if eng == "V":
                nc.vector.tensor_copy(out=dst, in_=src)
            else:
                nc.scalar.copy(out=dst, in_=src)

        def keep_clock(pt, n):
            for i in range(n):
                nc.tensor.matmul(out=pt[:, 0:P], lhsT=ident[:], rhs=ident[:], start=True, stop=True)

        bbt = psum.tile([P, 1024], BF16, tag="bbt")

        def bias_spread(h):
            nc.tensor.matmul(out=bbt[:, half(h)], lhsT=sel_b[:], rhs=zb[:, half(h)], start=True, stop=True)

        pns = {}

        def pn_mm(h):
            pns[h] = bank("pn%d" % h)
            nc.tensor.matmul(out=pns[h][:], lhsT=sel_n[:], rhs=z[:, half(h)], start=True, stop=True)

        def pn_copy(h):
            nc.scalar.copy(out=posb[2][:, half(h)], in_=pns[h][:])

        def posb_v(g, c0, c1):
            cols = slice(c0, c1)
            nc.vector.tensor_tensor(out=posb[g][:, cols], in0=bbt[:, cols], in1=pos_sb[g][:, cols], op=ADD)

        def regroup(s, t, eng="V", j0=0, j1=6):
            dst = v2[s][:].bitcast(F32).rearrange("p (j u t y x) -> p t j u y x", j=6, u=2, t=2, y=16)
            src = v_sb[t][:].bitcast(F32).rearrange("p (y j x u) -> p j u y x", y=16, j=6, u=2)
            for u in range(2):
                copy_out(eng, dst[:, t, j0:j1, u], src[:, j0:j1, u])

        def tok_a(j0, n=0):
            pt = bank("pa%d" % j0)
            keep_clock(pt, n)
            vw = v2[0][:].bitcast(F32)
            for i in range(4):
                r = 2 * j0 + i
                nc.tensor.transpose(pt[:, i * P:(i + 1) * P], vw[:, r * P:(r + 1) * P], perm_a[:])
            return pt[:].rearrange("p (j u i b d) -> p i b j d u", j=2, u=2, i=4, b=4)

        def tok_b(j0):
            pt = bank("pb%d" % j0)
            vw = v2[1][:].bitcast(F32)
            for i in range(4):
                r = 2 * j0 + i
                nc.tensor.transpose(pt[:, i * 64:i * 64 + P], vw[:, r * P:(r + 1) * P], perm_b[:])
            return pt[:, 0:256].rearrange("p (j u i b d) -> p i b j d u", j=2, u=2, i=2, b=4)

        g_l = grpw[:, 0:256].rearrange("p (b d r u) -> p b r d u", b=4, r=4, u=2)
        g_t = [grpw[:, 256 + g * 1024:1280 + g * 1024].rearrange("p (b r d u) -> p b r d u", b=4, r=16, u=2) for g in range(2)]

        def put(eng, src, i, r):
            if r < 4:
                dst = g_l[:, :, r:r + 2]
            else:
                g, r0 = (r - 4) // 16, (r - 4) % 16
                dst = g_t[g][:, :, r0:r0 + 2]
            copy_out(eng, dst, src[:, i])

        pws = {}

        def w_t(q, n=0):
            pws[q] = bank("pw%d" % q)
            keep_clock(pws[q], n)
            for i in range(4):
                a, u = i // 2, i % 2
                words = w_sb[:, q, a, :].bitcast(F32)
                nc.tensor.transpose(pws[q][:, i * P:(i + 1) * P], words[:, u:256:2], ident[:])

        def w_c(q, eng):
            copy_out(
                eng,
                gww[:, q * 512:(q + 1) * 512].rearrange("p (m a u) -> p m a u", a=2, u=2),
                pws[q][:].rearrange("p (a u m) -> p m a u", a=2, u=2),
            )

        def quant_tok(c0, n):
            nc.vector.quantize_mx(out=tokc[:, c0:c0 + n].bitcast(FP8X4), scales=toks[:, c0:c0 + n], in_=grp[:, 4 * c0:4 * (c0 + n)])

        def quant_w(c0, n):
            nc.vector.quantize_mx(out=wc[:, c0:c0 + n].bitcast(FP8X4), scales=ws[:, c0:c0 + n], in_=gw[:, 4 * c0:4 * (c0 + n)])

        def mx(t, h):
            acc = bank("acc%d_%d" % (t, h))
            nc.tensor.matmul_mx(
                out=acc[:],
                lhsT=tokc[:, t * P:(t + 1) * P].bitcast(FP8X4), lhsT_scale=toks[:, t * P:(t + 1) * P],
                rhs=wc[:, half(h)].bitcast(FP8X4), rhs_scale=ws[:, half(h)],
                start=True, stop=True,
            )
            accs[(t, h)] = acc

        def group_of(t):
            return 2 if t == 0 else (t - 1) // 4

        def add_v(t, h):
            nc.vector.tensor_tensor(out=o_sb[t][:, half(h)], in0=accs[(t, h)][:], in1=posb[group_of(t)][:, half(h)], op=ADD)

        def add_sg(t, h):
            tmp = keep.tile([P, 512], F32, name="tmp%d_%d" % (t, h))
            nc.scalar.copy(out=tmp[:], in_=accs[(t, h)][:])
            nc.gpsimd.tensor_tensor(out=o_sb[t][:, half(h)], in0=tmp[:], in1=posb[group_of(t)][:, half(h)], op=ADD)

        def dram(t, cols):
            if t == 0:
                return on[:, 0:4, cols]
            g, bi = (t - 1) // 4, (t - 1) % 4
            return ov[bi, 4 + 16 * g:20 + 16 * g, :, cols]

        def store(t, h=None):
            cols = slice(0, 1024) if h is None else half(h)
            nc.sync.dma_start(out=dram(t, cols), in_=o_sb[t][:, cols])

        keep_clock(bank("clock"), 4)
        bias_spread(0)
        bias_spread(1)
        regroup(0, 0)
        regroup(0, 1)
        posb_v(0, 0, 512)
        load_w(2, 4)
        load_b()
        load_pos(1)
        w_t(0, 0)
        a01 = tok_a(0, 0)
        w_c(0, "S")
        put("V", a01, 0, 0)
        put("V", a01, 1, 6)
        put("V", a01, 2, 12)
        put("V", a01, 3, 18)
        w_t(1, 1)
        quant_w(0, 256)
        a23 = tok_a(2, 0)
        w_c(1, "S")
        put("V", a23, 0, 2)
        quant_tok(0, 128)
        put("V", a23, 1, 8)
        put("V", a23, 2, 14)
        a45 = tok_a(4, 1)
        quant_w(256, 256)
        put("S", a45, 0, 4)
        put("S", a45, 1, 10)
        put("S", a45, 2, 16)
        put("V", a23, 3, 20)
        pn_mm(0)
        pn_copy(0)
        put("S", a45, 3, 22)
        w_t(2)
        mx(0, 0)
        quant_tok(128, 512)
        w_c(2, "S")
        w_t(3)
        add_v(0, 0)
        store(0, 0)
        regroup(1, 0)
        mx(1, 0)
        mx(2, 0)
        mx(3, 0)
        w_c(3, "S")
        add_v(1, 0)
        store(1, 0)
        quant_w(512, 512)
        mx(4, 0)
        pn_mm(1)
        add_sg(2, 0)
        add_v(3, 0)
        store(3, 0)
        regroup(1, 1, "S")
        pn_copy(1)
        mx(0, 1)
        add_v(4, 0)
        store(4, 0)
        posb_v(0, 512, 1024)
        mx(1, 1)
        store(2, 0)
        add_v(0, 1)
        store(0, 1)
        b01 = tok_b(0)
        b23 = tok_b(2)
        b45 = tok_b(4)
        put("S", b01, 0, 24)
        put("S", b01, 1, 30)
        put("S", b23, 0, 26)
        put("S", b23, 1, 32)
        put("S", b45, 0, 28)
        put("S", b45, 1, 34)
        mx(2, 1)
        mx(3, 1)
        add_v(1, 1)
        store(1, 1)
        quant_tok(640, 512)
        add_sg(2, 1)
        mx(4, 1)
        add_v(3, 1)
        store(3, 1)
        add_sg(4, 1)
        posb_v(1, 0, 512)
        mx(5, 0)
        mx(6, 0)
        store(2, 1)
        add_v(5, 0)
        store(5, 0)
        mx(7, 0)
        add_sg(6, 0)
        store(4, 1)
        mx(8, 0)
        mx(5, 1)
        add_v(7, 0)
        store(7, 0)
        mx(6, 1)
        add_v(8, 0)
        store(8, 0)
        store(6, 0)
        posb_v(1, 512, 1024)
        add_sg(6, 1)
        mx(7, 1)
        mx(8, 1)
        add_v(5, 1)
        store(5, 1)
        add_v(7, 1)
        store(7, 1)
        store(6, 1)
        add_v(8, 1)
        store(8, 1)
